import numpy as np
import ml_dtypes


def mxq(x, axis, fmt="e4m3"):
    dtype, down = {"e4m3": (ml_dtypes.float8_e4m3fn, 7), "e5m2": (ml_dtypes.float8_e5m2, 14)}[fmt]
    v = np.moveaxis(np.asarray(x, np.float32).astype(ml_dtypes.bfloat16).astype(np.float64), axis, -1)
    blocks = v.reshape(v.shape[:-1] + (-1, 32))
    amax = np.abs(blocks).max(-1, keepdims=True)
    byte = np.maximum(np.where(amax > 0, np.frexp(amax)[1] - 1 + 127, 0) - down, 1)
    scale = np.exp2(byte - 127.0)
    codes = (blocks / scale).astype(np.float32).astype(dtype).astype(np.float64)
    return np.moveaxis((codes * scale).reshape(v.shape), -1, axis)


WIDE = False


def mx_kscale(k):
    if not WIDE:
        return np.ones(k)
    levels = np.array([18, -18])
    if k % 512:
        return np.exp2(np.random.permutation(np.resize(levels, k // 32))).repeat(32)
    a = np.empty((k // 512, 16))
    for p in range(k // 512):
        a[p, :8] = np.random.permutation(np.resize(levels, 8))
        for g in range(8):
            far = levels[np.abs(levels - a[p, g]) >= 10]
            a[p, g + 8] = far[np.random.randint(len(far))]
    return np.exp2(a.ravel()).repeat(32)


BF16 = ml_dtypes.bfloat16


def bf(x):
    return np.asarray(x, np.float32).astype(BF16)


def f64(x):
    return np.asarray(x).astype(np.float64)


B, S, D, H, DK = 2, 256, 1024, 8, 128
HD = H * DK
T = B * S
EPS = 1e-6


def heads(v):
    return v.reshape(B, S, H, DK).transpose(0, 2, 1, 3)


def unheads(g):
    return g.transpose(0, 2, 1, 3).reshape(T, HD)


def setup_inputs():
    s = mx_kscale(T).reshape(B, S)
    uq = mx_kscale(HD)
    uk = mx_kscale(HD)
    uv = mx_kscale(HD)

    def w(u):
        return bf(f64(bf(np.random.standard_normal((D, HD)) / np.sqrt(D))) / u)

    def b():
        return bf(np.random.standard_normal(HD) * 0.1)

    def grad(u):
        e = np.exp2(np.random.randint(-6, 1, (B, 1, S, 1)))
        return bf(np.random.standard_normal((B, H, S, DK)) * e / s[:, None, :, None] * u.reshape(1, H, 1, DK))

    x0 = bf(np.random.standard_normal((B, S, D)))
    g1 = bf(1.0 + 0.1 * np.random.standard_normal(D))
    wq = w(uq)
    bq = b()
    wk = w(uk)
    bk = b()
    wv = w(uv)
    bv = b()
    g0 = grad(uq)
    gk = grad(uk)
    gv = grad(uv)
    x0f = f64(x0)
    rstd = 1.0 / np.sqrt(np.mean(x0f * x0f, axis=-1) + EPS)
    return {"x": bf(x0f * s[:, :, None]), "g1": g1, "wq": wq, "bq": bq, "wk": wk, "bk": bk, "wv": wv, "bv": bv,
            "rstd": np.asarray(rstd, np.float32), "grad_0": g0, "grad_1": gk, "grad_2": gv}


def reference(x, g1, wq, bq, wk, bk, wv, bv, rstd, grad_0, grad_1, grad_2):
    r = f64(rstd).reshape(T, 1)
    gain = f64(g1)
    xhat = f64(x).reshape(T, D) * r
    n = xhat * gain
    dz = np.concatenate([unheads(f64(grad_0)), unheads(f64(grad_1)), unheads(f64(grad_2))], axis=1)
    w = np.concatenate([f64(wq), f64(wk), f64(wv)], axis=1)
    dn = mxq(dz, 1, "e5m2") @ mxq(w, 1, "e4m3").T
    dw = mxq(n, 0, "e4m3").T @ mxq(dz, 0, "e5m2")
    dxhat = dn * gain
    dx = r * (dxhat - xhat * np.mean(dxhat * xhat, axis=1, keepdims=True))
    return dx.reshape(B, S, D), dw[:, :HD], dw[:, HD:2 * HD], dw[:, 2 * HD:]

@@ -1,0 +1,394 @@
+from contextlib import ExitStack
+
+import concourse.mybir as mybir
+from concourse.masks import make_identity
+
+B, S, D, H, DK = 2, 256, 1024, 8, 128
+T = B * S
+FLOPS = 2 * 2 * T * D * 3 * D
+BYTES = 2 * T * D + 2 * D + 3 * 2 * D * D + 4 * T + 3 * 2 * T * D + 4 * T * D + 3 * 4 * D * D
+
+F32 = mybir.dt.float32
+BF16 = mybir.dt.bfloat16
+U32 = mybir.dt.uint32
+I32 = mybir.dt.int32
+U8 = mybir.dt.uint8
+E4M3 = mybir.dt.float8_e4m3fn_x4
+E5M2 = mybir.dt.float8_e5m2_x4
+MULT = mybir.AluOpType.mult
+ADD = mybir.AluOpType.add
+
+P = 128
+PACK = 4
+W = 512
+HALF = 64
+
+
+def tile_transformerblock_pa_v_kernel(
+    tc, x, g1, wq, bq, wk, bk, wv, bv, rstd, grad_0, grad_1, grad_2, out_0, out_1, out_2, out_3
+):
+    nc = tc.nc
+    grads = [grad_0, grad_1, grad_2]
+    weights = [wq, wk, wv]
+    dws = [out_1, out_2, out_3]
+    ACT, DVE = nc.scalar, nc.vector
+
+    with ExitStack() as ctx:
+        keep = ctx.enter_context(tc.tile_pool(name="keep", bufs=1))
+        stage = ctx.enter_context(tc.tile_pool(name="stage", bufs=8))
+        outs = ctx.enter_context(tc.tile_pool(name="outs", bufs=9))
+        psum = ctx.enter_context(tc.psum_pool(name="psum", bufs=8))
+        ctx.enter_context(tc.manual_schedule())
+
+        def copy(engine, out, in_):
+            if engine is ACT:
+                nc.scalar.copy(out=out, in_=in_)
+            else:
+                nc.vector.tensor_copy(out=out, in_=in_)
+
+        def staged(name):
+            return stage.tile([P, PACK * W], BF16, name=name, tag="stage", align_bytes=64)
+
+        def bank(name):
+            return psum.tile([P, W], F32, name=name, tag="bank")
+
+        def quantised(name):
+            codes = keep.tile([P, W], U32, name=name + "_codes", align_bytes=64)
+            scales = keep.tile([P, W], U8, name=name + "_scales", align_bytes=64)
+            return codes, scales
+
+        ident = keep.tile([P, P], F32)
+        make_identity(nc, ident[:])
+
+        r_sb = keep.tile([P, PACK], F32)
+        g_col = keep.tile([P, D // P], BF16)
+        x_sb = keep.tile([P, PACK, D], BF16)
+        dz_raw = {}
+        w_raw = {}
+
+        def load_small():
+            nc.sync.dma_start(out=g_col[:], in_=g1.rearrange("(p c) -> p c", p=P))
+            nc.sync.dma_start(out=r_sb[:], in_=rstd.rearrange("b (q j) -> (b q) j", j=PACK))
+
+        def load_x():
+            nc.sync.dma_start(out=x_sb[:], in_=x.rearrange("b (q j) d -> (b q) j d", j=PACK))
+
+        def load_dz(g0, n, queues):
+            i, h0 = divmod(g0, 2)
+            raw = keep.tile([P, n * 4, PACK * DK], BF16, name="dz_raw%d" % g0)
+            for b in range(B):
+                src = grads[i][b, 4 * h0 : 4 * (h0 + n)].rearrange("h (q j) k -> q h (j k)", j=PACK)
+                queues[b].dma_start(out=raw[HALF * b : HALF * (b + 1)], in_=src)
+            for s in range(n):
+                dz_raw[g0 + s] = raw[:, 4 * s : 4 * (s + 1), :]
+
+        def load_w(l):
+            dh, i = divmod(l, 3)
+            raw = keep.tile([P, 2, 2 * D], BF16, name="w_raw%d" % l)
+            src = weights[i][W * dh : W * (dh + 1), :].rearrange("(a p c) f -> p a (c f)", a=2, c=2)
+            nc.sync.dma_start(out=raw[:], in_=src)
+            w_raw[l] = raw
+
+        g_row = keep.tile([P, D], BF16)
+        neg_r2 = keep.tile([P, PACK], F32)
+
+        def spread_gain():
+            words = g_col[:].bitcast(F32)
+            acc = bank("g_bank")
+            for c in range(4):
+                nc.tensor.transpose(acc[:, P * c : P * (c + 1)], words[:, c : c + 1].to_broadcast([P, P]), ident[:])
+            nc.scalar.copy(
+                out=g_row[:].bitcast(F32).rearrange("p (n c) -> p n c", c=4),
+                in_=acc[:].rearrange("p (c n) -> p n c", c=4),
+            )
+
+        def row_factor():
+            nc.vector.scalar_tensor_tensor(
+                out=neg_r2[:], in0=r_sb[:], scalar=-1.0 / D, in1=r_sb[:], op0=MULT, op1=MULT
+            )
+
+        st = {}
+        q = {}
+
+        def quantise(key, fmt):
+            codes, scales = quantised("q_%s%d" % key)
+            nc.vector.quantize_mx(out=codes[:].bitcast(fmt), scales=scales[:], in_=st.pop(key)[:])
+            q[key] = (codes, scales)
+
+        def A(g, engine=DVE):
+            t = staged("dz_tok")
+            copy(
+                engine,
+                t[:].rearrange("p (h c i j) -> p h c j i", h=4, i=4, j=PACK),
+                dz_raw[g].rearrange("p h (j c i) -> p h c j i", j=PACK, i=4),
+            )
+            st[("a", g)] = t
+
+        def QA(g):
+            quantise(("a", g), E5M2)
+
+        def N(dh):
+            t = staged("n_rows")
+            cols = slice(W * dh, W * (dh + 1))
+            for j in range(PACK):
+                nc.vector.scalar_tensor_tensor(
+                    out=t[:, W * j : W * (j + 1)],
+                    in0=x_sb[:, j, cols],
+                    scalar=r_sb[:, j : j + 1],
+                    in1=g_row[:, cols],
+                    op0=MULT,
+                    op1=MULT,
+                )
+            st[("nb", dh)] = t
+
+        def NI(dh, engine=DVE):
+            t = staged("n_tok")
+            copy(
+                engine,
+                t[:].rearrange("p (c i j) -> p c j i", i=4, j=PACK),
+                st.pop(("nb", dh))[:].rearrange("p (j c i) -> p c j i", j=PACK, i=4),
+            )
+            st[("n", dh)] = t
+
+        def QN(dh):
+            quantise(("n", dh), E4M3)
+
+        def F(g, engine=DVE):
+            t = staged("dz_sorted")
+            dt = U32 if engine is ACT else I32
+            copy(
+                engine,
+                t[:].bitcast(dt).rearrange("p (j u h w) -> p j u h w", j=PACK, u=2, h=4),
+                dz_raw[g].bitcast(dt).rearrange("p h (j w u) -> p j u h w", j=PACK, u=2),
+            )
+            st[("f", g)] = t
+
+        def TZ(g, engine=ACT):
+            words = st.pop(("f", g))[:].bitcast(F32)
+            t = staged("dz_feat")
+            dst = t[:].bitcast(F32)
+            for pair in range(2):
+                acc = bank("dz_bank")
+                for s in range(4):
+                    c0 = W * pair + P * s
+                    nc.tensor.transpose(acc[:, P * s : P * (s + 1)], words[:, c0 : c0 + P], ident[:])
+                copy(
+                    engine,
+                    dst[:, W * pair : W * (pair + 1)].rearrange("p (j m u) -> p j m u", j=2, u=2),
+                    acc[:].rearrange("p (j u m) -> p j m u", j=2, u=2),
+                )
+            st[("z", g)] = t
+
+        def QT(g):
+            quantise(("z", g), E5M2)
+
+        def TW(u, engine=ACT):
+            l, h = divmod(u, 2)
+            words = w_raw[l][:].bitcast(F32)
+            t = staged("w_feat")
+            dst = t[:].bitcast(F32)
+            for a in range(2):
+                acc = bank("w_bank")
+                for c in range(2):
+                    for e in range(2):
+                        c0 = W * c + 256 * h
+                        s = 2 * c + e
+                        nc.tensor.transpose(acc[:, P * s : P * (s + 1)], words[:, a, c0 + e : c0 + 256 : 2], ident[:])
+                copy(
+                    engine,
+                    dst[:, W * a : W * (a + 1)].rearrange("p (m s) -> p m s", s=4),
+                    acc[:].rearrange("p (s m) -> p m s", s=4),
+                )
+            st[("w", u)] = t
+
+        def QW(u):
+            quantise(("w", u), E4M3)
+
+        def mx(acc, lhs, lhs_fmt, cols, rhs, rhs_fmt, start, stop):
+            nc.tensor.matmul_mx(
+                out=acc[:],
+                lhsT=lhs[0][:, cols].bitcast(lhs_fmt),
+                lhsT_scale=lhs[1][:, cols],
+                rhs=rhs[0][:].bitcast(rhs_fmt),
+                rhs_scale=rhs[1][:],
+                start=start,
+                stop=stop,
+            )
+
+        def DW(k, engines=(ACT, ACT)):
+            i, dt = divmod(k, 8)
+            dh, m = divmod(dt, 4)
+            res = outs.tile([P, D], F32, name="res", tag="res")
+            accs = []
+            for h in range(2):
+                acc = bank("dw_bank")
+                mx(acc, q[("n", dh)], E4M3, slice(P * m, P * (m + 1)), q[("a", 2 * i + h)], E5M2, True, True)
+                accs.append(acc)
+            for h in range(2):
+                copy(engines[h], res[:, W * h : W * (h + 1)], accs[h][:])
+            nc.sync.dma_start(out=dws[i][P * dt : P * (dt + 1), :], in_=res[:])
+
+        dn = {}
+        tt = [keep.tile([P, D], F32, name="t%d" % j) for j in range(PACK)]
+        cc = keep.tile([P, PACK], F32)
+        dx = {}
+
+        def MN(j, dh):
+            acc = bank("dn_bank")
+            for g in range(6):
+                mx(acc, q[("z", g)], E5M2, slice(P * j, P * (j + 1)), q[("w", 6 * dh + g)], E4M3, g == 0, g == 5)
+            dn[(j, dh)] = acc
+
+        def E1(j, dh):
+            cols = slice(W * dh, W * (dh + 1))
+            nc.vector.scalar_tensor_tensor(
+                out=tt[j][:, cols],
+                in0=dn.pop((j, dh))[:],
+                scalar=r_sb[:, j : j + 1],
+                in1=g_row[:, cols],
+                op0=MULT,
+                op1=MULT,
+            )
+
+        def E2(j):
+            res = outs.tile([P, D], F32, name="res", tag="res")
+            nc.vector.scalar_tensor_tensor(
+                out=res[:],
+                in0=tt[j][:],
+                scalar=neg_r2[:, j : j + 1],
+                in1=x_sb[:, j, :],
+                op0=MULT,
+                op1=MULT,
+                accum_out=cc[:, j : j + 1],
+            )
+            dx[j] = res
+
+        def E3(j):
+            res = dx.pop(j)
+            nc.vector.scalar_tensor_tensor(
+                out=res[:], in0=x_sb[:, j, :], scalar=cc[:, j : j + 1], in1=tt[j][:], op0=MULT, op1=ADD
+            )
+            nc.sync.dma_start(out=out_0.rearrange("b (q j) d -> (b q) j d", j=PACK)[:, j, :], in_=res[:])
+
+        load_small()
+        load_dz(0, 1, (nc.sync, nc.sync))
+        load_dz(1, 1, (nc.sync, nc.sync))
+        load_w(0)
+        load_x()
+        load_dz(2, 2, (nc.sync, nc.sync))
+        load_w(1)
+        load_dz(4, 2, (nc.sync, nc.sync))
+        load_w(2)
+        load_w(3)
+        load_w(4)
+        load_w(5)
+        spread_gain()
+        F(0)
+        A(0)
+        TZ(0)
+        F(1)
+        QA(0)
+        TZ(1)
+        A(1)
+        QT(0)
+        QA(1)
+        QT(1)
+        row_factor()
+        TW(0)
+        TW(1)
+        N(0)
+        QW(0)
+        NI(0, ACT)
+        QW(1)
+        F(2)
+        F(3)
+        QN(0)
+        TZ(2)
+        TZ(3)
+        DW(0)
+        TW(2)
+        TW(3)
+        N(1)
+        QT(2)
+        F(4)
+        F(5)
+        QT(3)
+        NI(1)
+        QW(2)
+        QN(1)
+        QW(3)
+        TZ(4)
+        TZ(5)
+        DW(1)
+        TW(4)
+        TW(5)
+        QT(4)
+        QT(5)
+        QW(4)
+        QW(5)
+        A(2)
+        DW(2)
+        DW(3)
+        MN(0, 0)
+        QA(2)
+        A(3)
+        E1(0, 0)
+        QA(3)
+        DW(4)
+        DW(5)
+        TW(6)
+        TW(7)
+        QW(6)
+        QW(7)
+        DW(6)
+        DW(7)
+        MN(1, 0)
+        A(4)
+        E1(1, 0)
+        QA(4)
+        DW(8)
+        DW(9)
+        TW(8)
+        TW(9, DVE)
+        QW(8)
+        QW(9)
+        DW(10)
+        DW(11)
+        MN(2, 0)
+        A(5)
+        E1(2, 0)
+        QA(5)
+        DW(12)
+        DW(13)
+        TW(10)
+        TW(11, DVE)
+        QW(10)
+        QW(11)
+        DW(14)
+        DW(15)
+        MN(3, 0)
+        E1(3, 0)
+        MN(0, 1)
+        DW(16)
+        DW(17)
+        E1(0, 1)
+        E2(0)
+        MN(1, 1)
+        DW(18)
+        DW(19)
+        E1(1, 1)
+        E3(0)
+        E2(1)
+        MN(2, 1)
+        DW(20)
+        DW(21)
+        E1(2, 1)
+        E3(1)
+        E2(2)
+        MN(3, 1)
+        DW(22)
+        DW(23)
+        E1(3, 1)
+        E3(2)
+        E2(3)
+        E3(3)

@@ -35,7 +35,9 @@ def tile_transformerblock_pa_v_kernel(
 
     with ExitStack() as ctx:
         keep = ctx.enter_context(tc.tile_pool(name="keep", bufs=1))
-        stage = ctx.enter_context(tc.tile_pool(name="stage", bufs=8))
+        stage = ctx.enter_context(tc.tile_pool(name="stage", bufs=6))
+        wide = ctx.enter_context(tc.tile_pool(name="wide", bufs=3))
+        rows = ctx.enter_context(tc.tile_pool(name="rows", bufs=2))
         outs = ctx.enter_context(tc.tile_pool(name="outs", bufs=9))
         psum = ctx.enter_context(tc.psum_pool(name="psum", bufs=8))
         ctx.enter_context(tc.manual_schedule())
@@ -62,31 +64,39 @@ def tile_transformerblock_pa_v_kernel(
 
         r_sb = keep.tile([P, PACK], F32)
         g_col = keep.tile([P, D // P], BF16)
-        x_sb = keep.tile([P, PACK, D], BF16)
-        dz_raw = {}
+        x_sb = [keep.tile([P, PACK, W], BF16, name="x%d" % dh) for dh in range(2)]
+        dz_raw = keep.tile([P, 3 * H, PACK * DK], BF16)
         w_raw = {}
+        queues = (nc.sync, nc.scalar)
+
+        def load_halves(dst, srcs):
+            for b in range(2):
+                queues[b].dma_start(out=dst[HALF * b : HALF * (b + 1)], in_=srcs[b])
 
         def load_small():
             nc.sync.dma_start(out=g_col[:], in_=g1.rearrange("(p c) -> p c", p=P))
-            nc.sync.dma_start(out=r_sb[:], in_=rstd.rearrange("b (q j) -> (b q) j", j=PACK))
+            nc.scalar.dma_start(out=r_sb[:], in_=rstd.rearrange("b (q j) -> (b q) j", j=PACK))
 
-        def load_x():
-            nc.sync.dma_start(out=x_sb[:], in_=x.rearrange("b (q j) d -> (b q) j d", j=PACK))
+        def load_x(dh):
+            cols = slice(W * dh, W * (dh + 1))
+            load_halves(x_sb[dh], [x[b, :, cols].rearrange("(q j) d -> q j d", j=PACK) for b in range(B)])
 
-        def load_dz(g0, n, queues):
+        def load_dz(g0, n):
             i, h0 = divmod(g0, 2)
-            raw = keep.tile([P, n * 4, PACK * DK], BF16, name="dz_raw%d" % g0)
-            for b in range(B):
-                src = grads[i][b, 4 * h0 : 4 * (h0 + n)].rearrange("h (q j) k -> q h (j k)", j=PACK)
-                queues[b].dma_start(out=raw[HALF * b : HALF * (b + 1)], in_=src)
-            for s in range(n):
-                dz_raw[g0 + s] = raw[:, 4 * s : 4 * (s + 1), :]
+            heads = slice(4 * h0, 4 * (h0 + n))
+            load_halves(
+                dz_raw[:, 4 * g0 : 4 * (g0 + n), :],
+                [grads[i][b, heads].rearrange("h (q j) k -> q h (j k)", j=PACK) for b in range(B)],
+            )
 
-        def load_w(l):
+        def load_w(l, split):
             dh, i = divmod(l, 3)
             raw = keep.tile([P, 2, 2 * D], BF16, name="w_raw%d" % l)
             src = weights[i][W * dh : W * (dh + 1), :].rearrange("(a p c) f -> p a (c f)", a=2, c=2)
-            nc.sync.dma_start(out=raw[:], in_=src)
+            if split:
+                load_halves(raw, [src[:HALF], src[HALF:]])
+            else:
+                nc.sync.dma_start(out=raw[:], in_=src)
             w_raw[l] = raw
 
         g_row = keep.tile([P, D], BF16)
@@ -120,7 +130,7 @@ def tile_transformerblock_pa_v_kernel(
             copy(
                 engine,
                 t[:].rearrange("p (h c i j) -> p h c j i", h=4, i=4, j=PACK),
-                dz_raw[g].rearrange("p h (j c i) -> p h c j i", j=PACK, i=4),
+                dz_raw[:, 4 * g : 4 * (g + 1), :].rearrange("p h (j c i) -> p h c j i", j=PACK, i=4),
             )
             st[("a", g)] = t
 
@@ -133,7 +143,7 @@ def tile_transformerblock_pa_v_kernel(
             for j in range(PACK):
                 nc.vector.scalar_tensor_tensor(
                     out=t[:, W * j : W * (j + 1)],
-                    in0=x_sb[:, j, cols],
+                    in0=x_sb[dh][:, j, :],
                     scalar=r_sb[:, j : j + 1],
                     in1=g_row[:, cols],
                     op0=MULT,
@@ -153,34 +163,39 @@ def tile_transformerblock_pa_v_kernel(
         def QN(dh):
             quantise(("n", dh), E4M3)
 
-        def F(g, engine=DVE):
-            t = staged("dz_sorted")
-            dt = U32 if engine is ACT else I32
-            copy(
-                engine,
-                t[:].bitcast(dt).rearrange("p (j u h w) -> p j u h w", j=PACK, u=2, h=4),
-                dz_raw[g].bitcast(dt).rearrange("p h (j w u) -> p j u h w", j=PACK, u=2),
+        def FJ(j):
+            t = wide.tile([P, 6 * W], BF16, name="dz_sorted", tag="wide", align_bytes=64)
+            nc.vector.tensor_copy(
+                out=t[:].bitcast(I32).rearrange("p (g u h w) -> p g u h w", g=6, u=2, h=4),
+                in_=dz_raw[:].bitcast(I32).rearrange("p (g h) (j w u) -> p j g u h w", h=4, j=PACK, u=2)[:, j],
             )
-            st[("f", g)] = t
+            st[("f", j)] = t
 
-        def TZ(g, engine=ACT):
-            words = st.pop(("f", g))[:].bitcast(F32)
-            t = staged("dz_feat")
+        def TZJ(j, engine=ACT):
+            words = st.pop(("f", j))[:].bitcast(F32)
+            t = wide.tile([P, 6 * W], BF16, name="dz_feat", tag="wide", align_bytes=64)
             dst = t[:].bitcast(F32)
-            for pair in range(2):
+            for pair in range(3):
                 acc = bank("dz_bank")
                 for s in range(4):
                     c0 = W * pair + P * s
                     nc.tensor.transpose(acc[:, P * s : P * (s + 1)], words[:, c0 : c0 + P], ident[:])
                 copy(
                     engine,
-                    dst[:, W * pair : W * (pair + 1)].rearrange("p (j m u) -> p j m u", j=2, u=2),
-                    acc[:].rearrange("p (j u m) -> p j m u", j=2, u=2),
+                    dst[:, W * pair : W * (pair + 1)].rearrange("p (g m u) -> p g m u", g=2, u=2),
+                    acc[:].rearrange("p (g u m) -> p g m u", g=2, u=2),
                 )
-            st[("z", g)] = t
+            st[("z", j)] = t
 
-        def QT(g):
-            quantise(("z", g), E5M2)
+        def QTJ(j):
+            t = st.pop(("z", j))
+            codes = keep.tile([P, 6 * P], U32, name="z_codes%d" % j, align_bytes=64)
+            scales = keep.tile([P, 6 * P], U8, name="z_scales%d" % j, align_bytes=64)
+            for lo, hi in ((0, 4 * P), (4 * P, 6 * P)):
+                nc.vector.quantize_mx(
+                    out=codes[:, lo:hi].bitcast(E5M2), scales=scales[:, lo:hi], in_=t[:, PACK * lo : PACK * hi]
+                )
+            q[("z", j)] = (codes, scales)
 
         def TW(u, engine=ACT):
             l, h = divmod(u, 2)
@@ -215,32 +230,39 @@ def tile_transformerblock_pa_v_kernel(
                 stop=stop,
             )
 
-        def DW(k, engines=(ACT, ACT)):
+        dw_res = {}
+
+        def DH(k, h, engine=ACT):
             i, dt = divmod(k, 8)
             dh, m = divmod(dt, 4)
-            res = outs.tile([P, D], F32, name="res", tag="res")
-            accs = []
-            for h in range(2):
-                acc = bank("dw_bank")
-                mx(acc, q[("n", dh)], E4M3, slice(P * m, P * (m + 1)), q[("a", 2 * i + h)], E5M2, True, True)
-                accs.append(acc)
-            for h in range(2):
-                copy(engines[h], res[:, W * h : W * (h + 1)], accs[h][:])
-            nc.sync.dma_start(out=dws[i][P * dt : P * (dt + 1), :], in_=res[:])
+            if h == 0:
+                dw_res[k] = outs.tile([P, D], F32, name="res", tag="res")
+            acc = bank("dw_bank")
+            mx(acc, q[("n", dh)], E4M3, slice(P * m, P * (m + 1)), q[("a", 2 * i + h)], E5M2, True, True)
+            copy(engine, dw_res[k][:, W * h : W * (h + 1)], acc[:])
+            if h == 1:
+                nc.sync.dma_start(out=dws[i][P * dt : P * (dt + 1), :], in_=dw_res.pop(k)[:])
+
+        def DW(k, engine=ACT):
+            DH(k, 0, engine)
+            DH(k, 1, engine)
 
         dn = {}
-        tt = [keep.tile([P, D], F32, name="t%d" % j) for j in range(PACK)]
+        tt = {}
         cc = keep.tile([P, PACK], F32)
+        part = keep.tile([P, PACK, 2], F32)
         dx = {}
 
-        def MN(j, dh):
+        def MJ(j, dh):
             acc = bank("dn_bank")
             for g in range(6):
-                mx(acc, q[("z", g)], E5M2, slice(P * j, P * (j + 1)), q[("w", 6 * dh + g)], E4M3, g == 0, g == 5)
+                mx(acc, q[("z", j)], E5M2, slice(P * g, P * (g + 1)), q[("w", 6 * dh + g)], E4M3, g == 0, g == 5)
             dn[(j, dh)] = acc
 
         def E1(j, dh):
             cols = slice(W * dh, W * (dh + 1))
+            if dh == 0:
+                tt[j] = rows.tile([P, D], F32, name="t", tag="t")
             nc.vector.scalar_tensor_tensor(
                 out=tt[j][:, cols],
                 in0=dn.pop((j, dh))[:],
@@ -250,145 +272,164 @@ def tile_transformerblock_pa_v_kernel(
                 op1=MULT,
             )
 
-        def E2(j):
-            res = outs.tile([P, D], F32, name="res", tag="res")
+        def E2(j, dh):
+            cols = slice(W * dh, W * (dh + 1))
+            if dh == 0:
+                dx[j] = outs.tile([P, D], F32, name="res", tag="res")
             nc.vector.scalar_tensor_tensor(
-                out=res[:],
-                in0=tt[j][:],
+                out=dx[j][:, cols],
+                in0=tt[j][:, cols],
                 scalar=neg_r2[:, j : j + 1],
-                in1=x_sb[:, j, :],
+                in1=x_sb[dh][:, j, :],
                 op0=MULT,
                 op1=MULT,
-                accum_out=cc[:, j : j + 1],
+                accum_out=part[:, j, dh : dh + 1],
             )
-            dx[j] = res
 
-        def E3(j):
-            res = dx.pop(j)
+        def EA(j):
+            nc.vector.tensor_tensor(out=cc[:, j : j + 1], in0=part[:, j, 0:1], in1=part[:, j, 1:2], op=ADD)
+
+        def E3(j, dh):
+            cols = slice(W * dh, W * (dh + 1))
             nc.vector.scalar_tensor_tensor(
-                out=res[:], in0=x_sb[:, j, :], scalar=cc[:, j : j + 1], in1=tt[j][:], op0=MULT, op1=ADD
+                out=dx[j][:, cols],
+                in0=x_sb[dh][:, j, :],
+                scalar=cc[:, j : j + 1],
+                in1=tt[j][:, cols],
+                op0=MULT,
+                op1=ADD,
             )
-            nc.sync.dma_start(out=out_0.rearrange("b (q j) d -> (b q) j d", j=PACK)[:, j, :], in_=res[:])
+            if dh == 1:
+                nc.sync.dma_start(out=out_0.rearrange("b (q j) d -> (b q) j d", j=PACK)[:, j, :], in_=dx.pop(j)[:])
 
         load_small()
-        load_dz(0, 1, (nc.sync, nc.sync))
-        load_dz(1, 1, (nc.sync, nc.sync))
-        load_w(0)
-        load_x()
-        load_dz(2, 2, (nc.sync, nc.sync))
-        load_w(1)
-        load_dz(4, 2, (nc.sync, nc.sync))
-        load_w(2)
-        load_w(3)
-        load_w(4)
-        load_w(5)
+        load_x(0)
+        load_dz(0, 1)
+        load_w(0, True)
         spread_gain()
-        F(0)
-        A(0)
-        TZ(0)
-        F(1)
-        QA(0)
-        TZ(1)
-        A(1)
-        QT(0)
-        QA(1)
-        QT(1)
-        row_factor()
-        TW(0)
-        TW(1)
+        load_dz(1, 1)
+        load_w(1, True)
+        load_x(1)
         N(0)
-        QW(0)
-        NI(0, ACT)
-        QW(1)
-        F(2)
-        F(3)
+        A(0, ACT)
+        load_dz(2, 2)
+        load_w(2, True)
+        NI(0)
+        TW(0)
+        load_dz(4, 2)
+        load_w(3, False)
+        load_w(4, False)
+        load_w(5, False)
+        QA(0)
         QN(0)
-        TZ(2)
-        TZ(3)
-        DW(0)
-        TW(2)
-        TW(3)
+        A(1)
+        QW(0)
+        QA(1)
+        row_factor()
+        DH(0, 0)
+        DH(1, 0)
+        TW(1)
+        DH(0, 1)
+        DH(1, 1)
         N(1)
-        QT(2)
-        F(4)
-        F(5)
-        QT(3)
+        QW(1)
         NI(1)
+        TW(2)
+        DW(2)
+        TW(3)
+        DW(3)
         QW(2)
         QN(1)
         QW(3)
-        TZ(4)
-        TZ(5)
-        DW(1)
-        TW(4)
-        TW(5)
-        QT(4)
-        QT(5)
-        QW(4)
-        QW(5)
         A(2)
-        DW(2)
-        DW(3)
-        MN(0, 0)
-        QA(2)
-        A(3)
-        E1(0, 0)
-        QA(3)
+        TW(4)
         DW(4)
+        TW(5)
         DW(5)
-        TW(6)
-        TW(7)
-        QW(6)
-        QW(7)
+        FJ(0)
+        QA(2)
+        FJ(1)
+        QW(4)
+        A(3)
+        QW(5)
+        TZJ(0)
         DW(6)
+        TZJ(1)
         DW(7)
-        MN(1, 0)
-        A(4)
-        E1(1, 0)
-        QA(4)
+        QA(3)
+        QTJ(0)
+        FJ(2)
+        QTJ(1)
+        TW(6)
+        MJ(0, 0)
+        TW(7)
         DW(8)
-        DW(9)
+        QW(6)
+        A(4)
+        E1(0, 0)
+        QA(4)
+        QW(7)
         TW(8)
-        TW(9, DVE)
+        MJ(1, 0)
+        TW(9)
+        DW(9)
+        DW(10, DVE)
         QW(8)
-        QW(9)
-        DW(10)
-        DW(11)
-        MN(2, 0)
+        E1(1, 0)
         A(5)
-        E1(2, 0)
+        QW(9)
         QA(5)
-        DW(12)
-        DW(13)
         TW(10)
-        TW(11, DVE)
+        DW(11)
+        DW(12, DVE)
+        TW(11)
+        DW(13)
+        DW(14, DVE)
         QW(10)
         QW(11)
-        DW(14)
+        TZJ(2)
         DW(15)
-        MN(3, 0)
-        E1(3, 0)
-        MN(0, 1)
+        FJ(3)
+        MJ(0, 1)
         DW(16)
+        TZJ(3)
         DW(17)
+        E2(0, 0)
         E1(0, 1)
-        E2(0)
-        MN(1, 1)
+        QTJ(2)
+        E2(0, 1)
+        MJ(1, 1)
         DW(18)
-        DW(19)
+        QTJ(3)
+        EA(0)
+        E2(1, 0)
+        E3(0, 0)
+        E3(0, 1)
         E1(1, 1)
-        E3(0)
-        E2(1)
-        MN(2, 1)
+        MJ(2, 0)
+        DW(19)
+        E1(2, 0)
+        E2(1, 1)
+        E2(2, 0)
+        EA(1)
+        MJ(2, 1)
         DW(20)
+        MJ(3, 0)
         DW(21)
         E1(2, 1)
-        E3(1)
-        E2(2)
-        MN(3, 1)
+        E3(1, 0)
+        E3(1, 1)
+        E2(2, 1)
+        E1(3, 0)
+        EA(2)
+        E2(3, 0)
         DW(22)
+        MJ(3, 1)
         DW(23)
+        E3(2, 0)
+        E3(2, 1)
         E1(3, 1)
-        E3(2)
-        E2(3)
-        E3(3)
+        E2(3, 1)
+        EA(3)
+        E3(3, 0)
+        E3(3, 1)

@@ -35,10 +35,12 @@ def tile_transformerblock_pa_v_kernel(
 
     with ExitStack() as ctx:
         keep = ctx.enter_context(tc.tile_pool(name="keep", bufs=1))
-        stage = ctx.enter_context(tc.tile_pool(name="stage", bufs=6))
+        stage = ctx.enter_context(tc.tile_pool(name="stage", bufs=8))
+        raws = ctx.enter_context(tc.tile_pool(name="raws", bufs=4))
+        small = ctx.enter_context(tc.tile_pool(name="small", bufs=2))
         wide = ctx.enter_context(tc.tile_pool(name="wide", bufs=3))
         rows = ctx.enter_context(tc.tile_pool(name="rows", bufs=2))
-        outs = ctx.enter_context(tc.tile_pool(name="outs", bufs=9))
+        outs = ctx.enter_context(tc.tile_pool(name="outs", bufs=10))
         psum = ctx.enter_context(tc.psum_pool(name="psum", bufs=8))
         ctx.enter_context(tc.manual_schedule())
 
@@ -65,39 +67,44 @@ def tile_transformerblock_pa_v_kernel(
         r_sb = keep.tile([P, PACK], F32)
         g_col = keep.tile([P, D // P], BF16)
         x_sb = [keep.tile([P, PACK, W], BF16, name="x%d" % dh) for dh in range(2)]
-        dz_raw = keep.tile([P, 3 * H, PACK * DK], BF16)
+        dz_raw = keep.tile([P, 6 * PACK * W], BF16)
         w_raw = {}
-        queues = (nc.sync, nc.scalar)
-
-        def load_halves(dst, srcs):
-            for b in range(2):
-                queues[b].dma_start(out=dst[HALF * b : HALF * (b + 1)], in_=srcs[b])
 
         def load_small():
             nc.sync.dma_start(out=g_col[:], in_=g1.rearrange("(p c) -> p c", p=P))
-            nc.scalar.dma_start(out=r_sb[:], in_=rstd.rearrange("b (q j) -> (b q) j", j=PACK))
+            nc.sync.dma_start(out=r_sb[:], in_=rstd.rearrange("b (q j) -> (b q) j", j=PACK))
 
         def load_x(dh):
-            cols = slice(W * dh, W * (dh + 1))
-            load_halves(x_sb[dh], [x[b, :, cols].rearrange("(q j) d -> q j d", j=PACK) for b in range(B)])
+            src = x.rearrange("b (q j) d -> (b q) j d", j=PACK)
+            nc.sync.dma_start(out=x_sb[dh][:], in_=src[:, :, W * dh : W * (dh + 1)])
 
-        def load_dz(g0, n):
-            i, h0 = divmod(g0, 2)
-            heads = slice(4 * h0, 4 * (h0 + n))
-            load_halves(
-                dz_raw[:, 4 * g0 : 4 * (g0 + n), :],
-                [grads[i][b, heads].rearrange("h (q j) k -> q h (j k)", j=PACK) for b in range(B)],
-            )
+        def slot(g, s):
+            c0 = PACK * W * g + 2 * W * s
+            return dz_raw[:, c0 : c0 + 2 * W]
 
-        def load_w(l, split):
+        def load_dz(g):
+            i, h0 = divmod(g, 2)
+            for b in range(B):
+                src = grads[i][b, 4 * h0 : 4 * (h0 + 1)].rearrange("(a s) (q j) k -> (s q) a (j k)", s=2, j=PACK)
+                nc.sync.dma_start(out=slot(g, b).rearrange("p (a c) -> p a c", a=2), in_=src)
+
+        def load_w(l):
             dh, i = divmod(l, 3)
-            raw = keep.tile([P, 2, 2 * D], BF16, name="w_raw%d" % l)
+            raw = raws.tile([P, 2, 2 * D], BF16, name="w_raw", tag="w_raw")
             src = weights[i][W * dh : W * (dh + 1), :].rearrange("(a p c) f -> p a (c f)", a=2, c=2)
-            if split:
-                load_halves(raw, [src[:HALF], src[HALF:]])
-            else:
-                nc.sync.dma_start(out=raw[:], in_=src)
+            nc.sync.dma_start(out=raw[:], in_=src)
             w_raw[l] = raw
+
+        parked = {}
+
+        def C12(g, engine=ACT):
+            tmp = small.tile([P, W], F32, name="parked", tag="parked")
+            copy(engine, tmp[:HALF], slot(g, 0).bitcast(F32)[HALF:])
+            copy(engine, slot(g, 0).bitcast(F32)[HALF:], slot(g, 1).bitcast(F32)[:HALF])
+            parked[g] = tmp
+
+        def C3(g):
+            nc.vector.tensor_copy(out=slot(g, 1).bitcast(F32)[:HALF], in_=parked.pop(g)[:HALF])
 
         g_row = keep.tile([P, D], BF16)
         neg_r2 = keep.tile([P, PACK], F32)
@@ -130,26 +137,28 @@ def tile_transformerblock_pa_v_kernel(
             copy(
                 engine,
                 t[:].rearrange("p (h c i j) -> p h c j i", h=4, i=4, j=PACK),
-                dz_raw[:, 4 * g : 4 * (g + 1), :].rearrange("p h (j c i) -> p h c j i", j=PACK, i=4),
+                dz_raw[:, PACK * W * g : PACK * W * (g + 1)].rearrange("p (h j c i) -> p h c j i", h=4, j=PACK, i=4),
             )
             st[("a", g)] = t
 
         def QA(g):
             quantise(("a", g), E5M2)
 
+        def NP(dh, j):
+            if j == 0:
+                st[("nb", dh)] = staged("n_rows")
+            nc.vector.scalar_tensor_tensor(
+                out=st[("nb", dh)][:, W * j : W * (j + 1)],
+                in0=x_sb[dh][:, j, :],
+                scalar=r_sb[:, j : j + 1],
+                in1=g_row[:, W * dh : W * (dh + 1)],
+                op0=MULT,
+                op1=MULT,
+            )
+
         def N(dh):
-            t = staged("n_rows")
-            cols = slice(W * dh, W * (dh + 1))
             for j in range(PACK):
-                nc.vector.scalar_tensor_tensor(
-                    out=t[:, W * j : W * (j + 1)],
-                    in0=x_sb[dh][:, j, :],
-                    scalar=r_sb[:, j : j + 1],
-                    in1=g_row[:, cols],
-                    op0=MULT,
-                    op1=MULT,
-                )
-            st[("nb", dh)] = t
+                NP(dh, j)
 
         def NI(dh, engine=DVE):
             t = staged("n_tok")
@@ -165,10 +174,10 @@ def tile_transformerblock_pa_v_kernel(
 
         def FJ(j):
             t = wide.tile([P, 6 * W], BF16, name="dz_sorted", tag="wide", align_bytes=64)
-            nc.vector.tensor_copy(
-                out=t[:].bitcast(I32).rearrange("p (g u h w) -> p g u h w", g=6, u=2, h=4),
-                in_=dz_raw[:].bitcast(I32).rearrange("p (g h) (j w u) -> p j g u h w", h=4, j=PACK, u=2)[:, j],
-            )
+            dst = t[:].bitcast(I32).rearrange("p (g u a s w) -> p u g a s w", g=6, u=2, a=2, s=2)
+            src = dz_raw[:].bitcast(I32).rearrange("p (g s a j w u) -> p j u g a s w", g=6, s=2, a=2, j=PACK, u=2)
+            for u in range(2):
+                nc.vector.tensor_copy(out=dst[:, u], in_=src[:, j, u])
             st[("f", j)] = t
 
         def TZJ(j, engine=ACT):
@@ -196,6 +205,31 @@ def tile_transformerblock_pa_v_kernel(
                     out=codes[:, lo:hi].bitcast(E5M2), scales=scales[:, lo:hi], in_=t[:, PACK * lo : PACK * hi]
                 )
             q[("z", j)] = (codes, scales)
+
+        def WS(u):
+            l, h = divmod(u, 2)
+            t = staged("w_sorted")
+            nc.vector.tensor_copy(
+                out=t[:].bitcast(I32).rearrange("p (r e m) -> p r e m", r=4, e=2),
+                in_=w_raw[l][:].bitcast(I32).rearrange("p a (c h m e) -> p h (a c) e m", c=2, h=2, e=2)[:, h],
+            )
+            st[("s", u)] = t
+
+        def TS(u, engine=ACT):
+            words = st.pop(("s", u))[:].bitcast(F32)
+            t = staged("w_feat")
+            dst = t[:].bitcast(F32)
+            for a in range(2):
+                acc = bank("w_bank")
+                for s in range(4):
+                    c0 = W * a + P * s
+                    nc.tensor.transpose(acc[:, P * s : P * (s + 1)], words[:, c0 : c0 + P], ident[:])
+                copy(
+                    engine,
+                    dst[:, W * a : W * (a + 1)].rearrange("p (m s) -> p m s", s=4),
+                    acc[:].rearrange("p (s m) -> p m s", s=4),
+                )
+            st[("w", u)] = t
 
         def TW(u, engine=ACT):
             l, h = divmod(u, 2)
@@ -239,7 +273,11 @@ def tile_transformerblock_pa_v_kernel(
                 dw_res[k] = outs.tile([P, D], F32, name="res", tag="res")
             acc = bank("dw_bank")
             mx(acc, q[("n", dh)], E4M3, slice(P * m, P * (m + 1)), q[("a", 2 * i + h)], E5M2, True, True)
-            copy(engine, dw_res[k][:, W * h : W * (h + 1)], acc[:])
+            copy(
+                engine,
+                dw_res[k][:, W * h : W * (h + 1)].rearrange("p (a s k) -> p s a k", a=2, s=2),
+                acc[:].rearrange("p (s a k) -> p s a k", s=2, a=2),
+            )
             if h == 1:
                 nc.sync.dma_start(out=dws[i][P * dt : P * (dt + 1), :], in_=dw_res.pop(k)[:])
 
@@ -304,132 +342,151 @@ def tile_transformerblock_pa_v_kernel(
 
         load_small()
         load_x(0)
-        load_dz(0, 1)
-        load_w(0, True)
-        spread_gain()
-        load_dz(1, 1)
-        load_w(1, True)
+        load_w(0)
+        load_dz(0)
+        load_dz(1)
         load_x(1)
+        load_dz(2)
+        load_w(1)
+        load_dz(3)
+        load_w(2)
+        load_dz(4)
+        load_dz(5)
+        load_w(3)
+        spread_gain()
         N(0)
-        A(0, ACT)
-        load_dz(2, 2)
-        load_w(2, True)
         NI(0)
-        TW(0)
-        load_dz(4, 2)
-        load_w(3, False)
-        load_w(4, False)
-        load_w(5, False)
-        QA(0)
+        C12(0,ACT)
+        C3(0)
         QN(0)
-        A(1)
-        QW(0)
-        QA(1)
+        A(0)
+        TW(0)
+        C12(1,ACT)
+        C3(1)
+        QA(0)
         row_factor()
-        DH(0, 0)
-        DH(1, 0)
+        A(1)
         TW(1)
-        DH(0, 1)
-        DH(1, 1)
-        N(1)
-        QW(1)
-        NI(1)
+        load_w(4)
+        C12(2,ACT)
+        NP(1,0)
+        QA(1)
+        NP(1,1)
+        NP(1,2)
+        NP(1,3)
+        DH(0,0)
+        DH(1,0)
+        C12(3,ACT)
+        DH(2,0)
+        DH(3,0)
         TW(2)
-        DW(2)
+        DH(0,1)
+        DH(1,1)
         TW(3)
-        DW(3)
-        QW(2)
+        load_w(5)
+        DH(2,1)
+        DH(3,1)
+        QW(0)
+        NI(1)
+        QW(1)
         QN(1)
-        QW(3)
-        A(2)
+        C3(2)
+        C3(3)
+        QW(2)
         TW(4)
         DW(4)
+        C12(4,ACT)
         TW(5)
-        DW(5)
-        FJ(0)
+        A(2)
+        QW(3)
         QA(2)
-        FJ(1)
+        DW(5,DVE)
+        C12(5,ACT)
         QW(4)
         A(3)
-        QW(5)
-        TZJ(0)
-        DW(6)
-        TZJ(1)
-        DW(7)
+        C3(4)
         QA(3)
-        QTJ(0)
-        FJ(2)
-        QTJ(1)
         TW(6)
-        MJ(0, 0)
+        DW(6)
         TW(7)
-        DW(8)
+        QW(5)
+        C3(5)
+        DW(7,DVE)
+        FJ(0)
         QW(6)
-        A(4)
-        E1(0, 0)
-        QA(4)
-        QW(7)
         TW(8)
-        MJ(1, 0)
+        DW(8)
         TW(9)
-        DW(9)
-        DW(10, DVE)
+        FJ(1)
+        QW(7)
+        DW(9,DVE)
         QW(8)
-        E1(1, 0)
-        A(5)
-        QW(9)
-        QA(5)
+        A(4)
+        TZJ(0)
+        DW(10)
         TW(10)
         DW(11)
-        DW(12, DVE)
         TW(11)
-        DW(13)
-        DW(14, DVE)
+        QW(9)
+        QTJ(0)
+        QA(4)
+        FJ(2)
         QW(10)
+        A(5)
         QW(11)
+        QA(5)
+        MJ(0,0)
+        TZJ(1)
+        DW(12)
+        E1(0,0)
+        FJ(3)
+        E2(0,0)
+        QTJ(1)
+        MJ(0,1)
+        DW(13)
+        DW(14)
         TZJ(2)
         DW(15)
-        FJ(3)
-        MJ(0, 1)
+        E1(0,1)
+        E2(0,1)
+        QTJ(2)
+        EA(0)
+        MJ(1,0)
         DW(16)
+        E1(1,0)
+        E3(0,0)
+        E2(1,0)
+        E3(0,1)
+        MJ(1,1)
         TZJ(3)
         DW(17)
-        E2(0, 0)
-        E1(0, 1)
-        QTJ(2)
-        E2(0, 1)
-        MJ(1, 1)
         DW(18)
+        E1(1,1)
         QTJ(3)
-        EA(0)
-        E2(1, 0)
-        E3(0, 0)
-        E3(0, 1)
-        E1(1, 1)
-        MJ(2, 0)
+        E2(1,1)
+        MJ(2,0)
         DW(19)
-        E1(2, 0)
-        E2(1, 1)
-        E2(2, 0)
+        E1(2,0)
         EA(1)
-        MJ(2, 1)
+        E2(2,0)
+        E3(1,0)
+        E3(1,1)
+        MJ(2,1)
         DW(20)
-        MJ(3, 0)
         DW(21)
-        E1(2, 1)
-        E3(1, 0)
-        E3(1, 1)
-        E2(2, 1)
-        E1(3, 0)
+        E1(2,1)
+        MJ(3,0)
+        E2(2,1)
+        E1(3,0)
         EA(2)
-        E2(3, 0)
+        E2(3,0)
+        E3(2,0)
+        MJ(3,1)
         DW(22)
-        MJ(3, 1)
+        E3(2,1)
         DW(23)
-        E3(2, 0)
-        E3(2, 1)
-        E1(3, 1)
-        E2(3, 1)
+        E1(3,1)
+        E2(3,1)
         EA(3)
-        E3(3, 0)
-        E3(3, 1)
+        E3(3,0)
+        E3(3,1)

@@ -20,8 +20,12 @@ ADD = mybir.AluOpType.add
 
 P = 128
 PACK = 4
-W = 512
-HALF = 64
+W = P * PACK
+BATCH_ROWS = P // B
+CHUNKS = 6
+SWAPPED = 4
+W_PIECES = 2 * CHUNKS
+VECTOR_DW_TILES = (5, 7, 9)
 
 
 def tile_transformerblock_pa_v_kernel(
@@ -31,231 +35,190 @@ def tile_transformerblock_pa_v_kernel(
     grads = [grad_0, grad_1, grad_2]
     weights = [wq, wk, wv]
     dws = [out_1, out_2, out_3]
-    ACT, DVE = nc.scalar, nc.vector
+    x_rows = x.rearrange("b (q j) d -> (b q) j d", j=PACK)
+    dx_rows = out_0.rearrange("b (q j) d -> (b q) j d", j=PACK)
 
     with ExitStack() as ctx:
         keep = ctx.enter_context(tc.tile_pool(name="keep", bufs=1))
+        w_loads = ctx.enter_context(tc.tile_pool(name="w_loads", bufs=4))
         stage = ctx.enter_context(tc.tile_pool(name="stage", bufs=8))
-        raws = ctx.enter_context(tc.tile_pool(name="raws", bufs=4))
-        small = ctx.enter_context(tc.tile_pool(name="small", bufs=2))
         wide = ctx.enter_context(tc.tile_pool(name="wide", bufs=3))
-        rows = ctx.enter_context(tc.tile_pool(name="rows", bufs=2))
-        outs = ctx.enter_context(tc.tile_pool(name="outs", bufs=10))
+        parking = ctx.enter_context(tc.tile_pool(name="parking", bufs=2))
+        scaled = ctx.enter_context(tc.tile_pool(name="scaled", bufs=2))
+        results = ctx.enter_context(tc.tile_pool(name="results", bufs=10))
         psum = ctx.enter_context(tc.psum_pool(name="psum", bufs=8))
         ctx.enter_context(tc.manual_schedule())
 
-        def copy(engine, out, in_):
-            if engine is ACT:
-                nc.scalar.copy(out=out, in_=in_)
-            else:
-                nc.vector.tensor_copy(out=out, in_=in_)
+        def half_cols(half):
+            return slice(W * half, W * (half + 1))
 
-        def staged(name):
-            return stage.tile([P, PACK * W], BF16, name=name, tag="stage", align_bytes=64)
+        def new_stage():
+            return stage.tile([P, PACK * W], BF16, name="staged", align_bytes=64)
 
-        def bank(name):
-            return psum.tile([P, W], F32, name=name, tag="bank")
+        def new_wide():
+            return wide.tile([P, CHUNKS * W], BF16, name="widened", align_bytes=64)
 
-        def quantised(name):
-            codes = keep.tile([P, W], U32, name=name + "_codes", align_bytes=64)
-            scales = keep.tile([P, W], U8, name=name + "_scales", align_bytes=64)
-            return codes, scales
+        def new_bank():
+            return psum.tile([P, W], F32, name="bank")
+
+        def new_result():
+            return results.tile([P, D], F32, name="result")
 
         ident = keep.tile([P, P], F32)
         make_identity(nc, ident[:])
 
-        r_sb = keep.tile([P, PACK], F32)
-        g_col = keep.tile([P, D // P], BF16)
-        x_sb = [keep.tile([P, PACK, W], BF16, name="x%d" % dh) for dh in range(2)]
-        dz_raw = keep.tile([P, 6 * PACK * W], BF16)
+        gain_col = keep.tile([P, D // P], BF16)
+        rstd_sb = keep.tile([P, PACK], F32)
+        x_sb = [keep.tile([P, PACK, W], BF16, name="x_half%d" % half) for half in range(2)]
+        dz_raw = keep.tile([P, CHUNKS * PACK * W], BF16)
         w_raw = {}
 
-        def load_small():
-            nc.sync.dma_start(out=g_col[:], in_=g1.rearrange("(p c) -> p c", p=P))
-            nc.sync.dma_start(out=r_sb[:], in_=rstd.rearrange("b (q j) -> (b q) j", j=PACK))
+        def parity_cols(c, s):
+            first = PACK * W * c + 2 * W * s
+            return dz_raw[:, first : first + 2 * W]
 
-        def load_x(dh):
-            src = x.rearrange("b (q j) d -> (b q) j d", j=PACK)
-            nc.sync.dma_start(out=x_sb[dh][:], in_=src[:, :, W * dh : W * (dh + 1)])
+        def load_x(half):
+            nc.sync.dma_start(out=x_sb[half][:], in_=x_rows[:, :, half_cols(half)])
 
-        def slot(g, s):
-            c0 = PACK * W * g + 2 * W * s
-            return dz_raw[:, c0 : c0 + 2 * W]
-
-        def load_dz(g):
-            i, h0 = divmod(g, 2)
+        def load_dz(c):
+            grad, first_head = grads[c // 2], 4 * (c % 2)
             for b in range(B):
-                src = grads[i][b, 4 * h0 : 4 * (h0 + 1)].rearrange("(a s) (q j) k -> (s q) a (j k)", s=2, j=PACK)
-                nc.sync.dma_start(out=slot(g, b).rearrange("p (a c) -> p a c", a=2), in_=src)
+                heads = grad[b, first_head : first_head + 4]
+                if c < SWAPPED:
+                    src = heads.rearrange("(a s) (q j) k -> (s q) a (j k)", s=2, j=PACK)
+                    nc.sync.dma_start(out=parity_cols(c, b).rearrange("p (a r) -> p a r", a=2), in_=src)
+                else:
+                    src = heads.rearrange("(a s) (q j) k -> s q a (j k)", s=2, j=PACK)
+                    rows = slice(BATCH_ROWS * b, BATCH_ROWS * (b + 1))
+                    for s in range(2):
+                        nc.sync.dma_start(out=parity_cols(c, s).rearrange("p (a r) -> p a r", a=2)[rows], in_=src[s])
 
-        def load_w(l):
-            dh, i = divmod(l, 3)
-            raw = raws.tile([P, 2, 2 * D], BF16, name="w_raw", tag="w_raw")
-            src = weights[i][W * dh : W * (dh + 1), :].rearrange("(a p c) f -> p a (c f)", a=2, c=2)
-            nc.sync.dma_start(out=raw[:], in_=src)
-            w_raw[l] = raw
+        def load_w(n):
+            half, i = divmod(n, 3)
+            w_raw[n] = w_loads.tile([P, 2, 2 * D], BF16, name="w_rows")
+            src = weights[i][half_cols(half), :].rearrange("(a p r) f -> p a (r f)", a=2, r=2)
+            nc.sync.dma_start(out=w_raw[n][:], in_=src)
 
         parked = {}
 
-        def C12(g, engine=ACT):
-            tmp = small.tile([P, W], F32, name="parked", tag="parked")
-            copy(engine, tmp[:HALF], slot(g, 0).bitcast(F32)[HALF:])
-            copy(engine, slot(g, 0).bitcast(F32)[HALF:], slot(g, 1).bitcast(F32)[:HALF])
-            parked[g] = tmp
+        def swap_out(c):
+            parked[c] = parking.tile([P, W], F32, name="parked")
+            even, odd = parity_cols(c, 0).bitcast(F32), parity_cols(c, 1).bitcast(F32)
+            nc.scalar.copy(out=parked[c][:BATCH_ROWS], in_=even[BATCH_ROWS:])
+            nc.scalar.copy(out=even[BATCH_ROWS:], in_=odd[:BATCH_ROWS])
 
-        def C3(g):
-            nc.vector.tensor_copy(out=slot(g, 1).bitcast(F32)[:HALF], in_=parked.pop(g)[:HALF])
+        def swap_in(c):
+            nc.vector.tensor_copy(out=parity_cols(c, 1).bitcast(F32)[:BATCH_ROWS], in_=parked.pop(c)[:BATCH_ROWS])
 
-        g_row = keep.tile([P, D], BF16)
-        neg_r2 = keep.tile([P, PACK], F32)
+        gain_row = keep.tile([P, D], BF16)
+        mean_factor = keep.tile([P, PACK], F32)
 
         def spread_gain():
-            words = g_col[:].bitcast(F32)
-            acc = bank("g_bank")
-            for c in range(4):
-                nc.tensor.transpose(acc[:, P * c : P * (c + 1)], words[:, c : c + 1].to_broadcast([P, P]), ident[:])
+            pairs = gain_col[:].bitcast(F32)
+            bank = new_bank()
+            for i in range(4):
+                nc.tensor.transpose(bank[:, P * i : P * (i + 1)], pairs[:, i : i + 1].to_broadcast([P, P]), ident[:])
             nc.scalar.copy(
-                out=g_row[:].bitcast(F32).rearrange("p (n c) -> p n c", c=4),
-                in_=acc[:].rearrange("p (c n) -> p n c", c=4),
+                out=gain_row[:].bitcast(F32).rearrange("p (m i) -> p m i", i=4),
+                in_=bank[:].rearrange("p (i m) -> p m i", i=4),
             )
 
-        def row_factor():
+        def make_mean_factor():
             nc.vector.scalar_tensor_tensor(
-                out=neg_r2[:], in0=r_sb[:], scalar=-1.0 / D, in1=r_sb[:], op0=MULT, op1=MULT
+                out=mean_factor[:], in0=rstd_sb[:], scalar=-1.0 / D, in1=rstd_sb[:], op0=MULT, op1=MULT
             )
 
-        st = {}
-        q = {}
+        pending = {}
+        quantised = {}
 
-        def quantise(key, fmt):
-            codes, scales = quantised("q_%s%d" % key)
-            nc.vector.quantize_mx(out=codes[:].bitcast(fmt), scales=scales[:], in_=st.pop(key)[:])
-            q[key] = (codes, scales)
+        def quantise(key, fmt, widths=(W,)):
+            src = pending.pop(key)
+            codes = keep.tile([P, sum(widths)], U32, name="codes_%s%d" % key, align_bytes=64)
+            scales = keep.tile([P, sum(widths)], U8, name="scales_%s%d" % key, align_bytes=64)
+            first = 0
+            for width in widths:
+                cols = slice(first, first + width)
+                nc.vector.quantize_mx(
+                    out=codes[:, cols].bitcast(fmt),
+                    scales=scales[:, cols],
+                    in_=src[:, PACK * first : PACK * (first + width)],
+                )
+                first = first + width
+            quantised[key] = (codes, scales)
 
-        def A(g, engine=DVE):
-            t = staged("dz_tok")
-            copy(
-                engine,
-                t[:].rearrange("p (h c i j) -> p h c j i", h=4, i=4, j=PACK),
-                dz_raw[:, PACK * W * g : PACK * W * (g + 1)].rearrange("p (h j c i) -> p h c j i", h=4, j=PACK, i=4),
+        def tokens_side_by_side(key, rows, groups):
+            pending[key] = new_stage()
+            nc.vector.tensor_copy(
+                out=pending[key][:].rearrange("p (g m i j) -> p g m j i", g=groups, i=4, j=PACK),
+                in_=rows.rearrange("p (g j m i) -> p g m j i", g=groups, j=PACK, i=4),
             )
-            st[("a", g)] = t
 
-        def QA(g):
-            quantise(("a", g), E5M2)
-
-        def NP(dh, j):
+        def normed_rows(half, j):
             if j == 0:
-                st[("nb", dh)] = staged("n_rows")
+                pending["n_rows", half] = new_stage()
             nc.vector.scalar_tensor_tensor(
-                out=st[("nb", dh)][:, W * j : W * (j + 1)],
-                in0=x_sb[dh][:, j, :],
-                scalar=r_sb[:, j : j + 1],
-                in1=g_row[:, W * dh : W * (dh + 1)],
+                out=pending["n_rows", half][:, W * j : W * (j + 1)],
+                in0=x_sb[half][:, j, :],
+                scalar=rstd_sb[:, j : j + 1],
+                in1=gain_row[:, half_cols(half)],
                 op0=MULT,
                 op1=MULT,
             )
 
-        def N(dh):
-            for j in range(PACK):
-                NP(dh, j)
+        def interleave_n(half):
+            tokens_side_by_side(("n", half), pending.pop(("n_rows", half))[:], 1)
 
-        def NI(dh, engine=DVE):
-            t = staged("n_tok")
-            copy(
-                engine,
-                t[:].rearrange("p (c i j) -> p c j i", i=4, j=PACK),
-                st.pop(("nb", dh))[:].rearrange("p (j c i) -> p c j i", j=PACK, i=4),
+        def interleave_dz(c):
+            tokens_side_by_side(("dz_tok", c), dz_raw[:, PACK * W * c : PACK * W * (c + 1)], 4)
+
+        def quantise_n(half):
+            quantise(("n", half), E4M3)
+
+        def quantise_dz_tok(c):
+            quantise(("dz_tok", c), E5M2)
+
+        def transpose_run(dst, sources):
+            for n in range(len(sources) // 4):
+                bank = new_bank()
+                for slot in range(4):
+                    nc.tensor.transpose(bank[:, P * slot : P * (slot + 1)], sources[4 * n + slot], ident[:])
+                nc.scalar.copy(
+                    out=dst[:].bitcast(F32)[:, W * n : W * (n + 1)].rearrange("p (i m e) -> p i m e", i=2, e=2),
+                    in_=bank[:].rearrange("p (i e m) -> p i m e", i=2, e=2),
+                )
+
+        def sort_dz_pairs(j):
+            pending["dz_sorted", j] = new_wide()
+            dst = pending["dz_sorted", j][:].bitcast(I32)
+            dst = dst.rearrange("p (c e a s v) -> p e c a s v", c=CHUNKS, e=2, a=2, s=2)
+            src = dz_raw[:].bitcast(I32).rearrange("p (c s a j v e) -> p j e c a s v", c=CHUNKS, s=2, a=2, j=PACK, e=2)
+            for e in range(2):
+                nc.vector.tensor_copy(out=dst[:, e], in_=src[:, j, e])
+
+        def transpose_dz(j):
+            pairs = pending.pop(("dz_sorted", j))[:].bitcast(F32)
+            pending["dz_feat", j] = new_wide()
+            transpose_run(pending["dz_feat", j], [pairs[:, P * i : P * (i + 1)] for i in range(2 * CHUNKS)])
+
+        def quantise_dz_feat(j):
+            quantise(("dz_feat", j), E5M2, (4 * P, 2 * P))
+
+        def transpose_w(u):
+            pairs = w_raw[u // 2][:].bitcast(F32)
+            firsts = [W * r + 2 * P * (u % 2) for r in range(2)]
+            pending["w", u] = new_stage()
+            transpose_run(
+                pending["w", u],
+                [pairs[:, a, first + e : first + 2 * P : 2] for a in range(2) for first in firsts for e in range(2)],
             )
-            st[("n", dh)] = t
 
-        def QN(dh):
-            quantise(("n", dh), E4M3)
-
-        def FJ(j):
-            t = wide.tile([P, 6 * W], BF16, name="dz_sorted", tag="wide", align_bytes=64)
-            dst = t[:].bitcast(I32).rearrange("p (g u a s w) -> p u g a s w", g=6, u=2, a=2, s=2)
-            src = dz_raw[:].bitcast(I32).rearrange("p (g s a j w u) -> p j u g a s w", g=6, s=2, a=2, j=PACK, u=2)
-            for u in range(2):
-                nc.vector.tensor_copy(out=dst[:, u], in_=src[:, j, u])
-            st[("f", j)] = t
-
-        def TZJ(j, engine=ACT):
-            words = st.pop(("f", j))[:].bitcast(F32)
-            t = wide.tile([P, 6 * W], BF16, name="dz_feat", tag="wide", align_bytes=64)
-            dst = t[:].bitcast(F32)
-            for pair in range(3):
-                acc = bank("dz_bank")
-                for s in range(4):
-                    c0 = W * pair + P * s
-                    nc.tensor.transpose(acc[:, P * s : P * (s + 1)], words[:, c0 : c0 + P], ident[:])
-                copy(
-                    engine,
-                    dst[:, W * pair : W * (pair + 1)].rearrange("p (g m u) -> p g m u", g=2, u=2),
-                    acc[:].rearrange("p (g u m) -> p g m u", g=2, u=2),
-                )
-            st[("z", j)] = t
-
-        def QTJ(j):
-            t = st.pop(("z", j))
-            codes = keep.tile([P, 6 * P], U32, name="z_codes%d" % j, align_bytes=64)
-            scales = keep.tile([P, 6 * P], U8, name="z_scales%d" % j, align_bytes=64)
-            for lo, hi in ((0, 4 * P), (4 * P, 6 * P)):
-                nc.vector.quantize_mx(
-                    out=codes[:, lo:hi].bitcast(E5M2), scales=scales[:, lo:hi], in_=t[:, PACK * lo : PACK * hi]
-                )
-            q[("z", j)] = (codes, scales)
-
-        def WS(u):
-            l, h = divmod(u, 2)
-            t = staged("w_sorted")
-            nc.vector.tensor_copy(
-                out=t[:].bitcast(I32).rearrange("p (r e m) -> p r e m", r=4, e=2),
-                in_=w_raw[l][:].bitcast(I32).rearrange("p a (c h m e) -> p h (a c) e m", c=2, h=2, e=2)[:, h],
-            )
-            st[("s", u)] = t
-
-        def TS(u, engine=ACT):
-            words = st.pop(("s", u))[:].bitcast(F32)
-            t = staged("w_feat")
-            dst = t[:].bitcast(F32)
-            for a in range(2):
-                acc = bank("w_bank")
-                for s in range(4):
-                    c0 = W * a + P * s
-                    nc.tensor.transpose(acc[:, P * s : P * (s + 1)], words[:, c0 : c0 + P], ident[:])
-                copy(
-                    engine,
-                    dst[:, W * a : W * (a + 1)].rearrange("p (m s) -> p m s", s=4),
-                    acc[:].rearrange("p (s m) -> p m s", s=4),
-                )
-            st[("w", u)] = t
-
-        def TW(u, engine=ACT):
-            l, h = divmod(u, 2)
-            words = w_raw[l][:].bitcast(F32)
-            t = staged("w_feat")
-            dst = t[:].bitcast(F32)
-            for a in range(2):
-                acc = bank("w_bank")
-                for c in range(2):
-                    for e in range(2):
-                        c0 = W * c + 256 * h
-                        s = 2 * c + e
-                        nc.tensor.transpose(acc[:, P * s : P * (s + 1)], words[:, a, c0 + e : c0 + 256 : 2], ident[:])
-                copy(
-                    engine,
-                    dst[:, W * a : W * (a + 1)].rearrange("p (m s) -> p m s", s=4),
-                    acc[:].rearrange("p (s m) -> p m s", s=4),
-                )
-            st[("w", u)] = t
-
-        def QW(u):
+        def quantise_w(u):
             quantise(("w", u), E4M3)
 
-        def mx(acc, lhs, lhs_fmt, cols, rhs, rhs_fmt, start, stop):
+        def mx_pass(bank, lhs, lhs_fmt, tile, rhs, rhs_fmt, start, stop):
+            cols = slice(P * tile, P * (tile + 1))
             nc.tensor.matmul_mx(
-                out=acc[:],
+                out=bank[:],
                 lhsT=lhs[0][:, cols].bitcast(lhs_fmt),
                 lhsT_scale=lhs[1][:, cols],
                 rhs=rhs[0][:].bitcast(rhs_fmt),
@@ -264,83 +227,90 @@ def tile_transformerblock_pa_v_kernel(
                 stop=stop,
             )
 
-        dw_res = {}
+        dw_tiles = {}
 
-        def DH(k, h, engine=ACT):
-            i, dt = divmod(k, 8)
-            dh, m = divmod(dt, 4)
-            if h == 0:
-                dw_res[k] = outs.tile([P, D], F32, name="res", tag="res")
-            acc = bank("dw_bank")
-            mx(acc, q[("n", dh)], E4M3, slice(P * m, P * (m + 1)), q[("a", 2 * i + h)], E5M2, True, True)
-            copy(
-                engine,
-                dw_res[k][:, W * h : W * (h + 1)].rearrange("p (a s k) -> p s a k", a=2, s=2),
-                acc[:].rearrange("p (s a k) -> p s a k", s=2, a=2),
-            )
-            if h == 1:
-                nc.sync.dma_start(out=dws[i][P * dt : P * (dt + 1), :], in_=dw_res.pop(k)[:])
+        def dw_half(k, side):
+            i, row_tile = divmod(k, 8)
+            half, tile = divmod(row_tile, 4)
+            if side == 0:
+                dw_tiles[k] = new_result()
+            bank = new_bank()
+            mx_pass(bank, quantised["n", half], E4M3, tile, quantised["dz_tok", 2 * i + side], E5M2, True, True)
+            dst = dw_tiles[k][:, half_cols(side)].rearrange("p (a s k) -> p s a k", a=2, s=2)
+            src = bank[:].rearrange("p (s a k) -> p s a k", s=2, a=2)
+            if k in VECTOR_DW_TILES:
+                nc.vector.tensor_copy(out=dst, in_=src)
+            else:
+                nc.scalar.copy(out=dst, in_=src)
 
-        def DW(k, engine=ACT):
-            DH(k, 0, engine)
-            DH(k, 1, engine)
+        def store_dw(k):
+            i, row_tile = divmod(k, 8)
+            nc.sync.dma_start(out=dws[i][P * row_tile : P * (row_tile + 1), :], in_=dw_tiles.pop(k)[:])
 
-        dn = {}
-        tt = {}
-        cc = keep.tile([P, PACK], F32)
-        part = keep.tile([P, PACK, 2], F32)
-        dx = {}
+        def dw_tile(k):
+            dw_half(k, 0)
+            dw_half(k, 1)
+            store_dw(k)
 
-        def MJ(j, dh):
-            acc = bank("dn_bank")
-            for g in range(6):
-                mx(acc, q[("z", j)], E5M2, slice(P * g, P * (g + 1)), q[("w", 6 * dh + g)], E4M3, g == 0, g == 5)
-            dn[(j, dh)] = acc
+        dn_banks = {}
+        dn_scaled = {}
+        dx_tiles = {}
+        row_parts = keep.tile([P, PACK, 2], F32)
+        row_terms = keep.tile([P, PACK], F32)
 
-        def E1(j, dh):
-            cols = slice(W * dh, W * (dh + 1))
-            if dh == 0:
-                tt[j] = rows.tile([P, D], F32, name="t", tag="t")
+        def dn_half(j, half):
+            dn_banks[j, half] = new_bank()
+            for c in range(CHUNKS):
+                w_piece = quantised["w", CHUNKS * half + c]
+                mx_pass(dn_banks[j, half], quantised["dz_feat", j], E5M2, c, w_piece, E4M3, c == 0, c == CHUNKS - 1)
+
+        def scale_dn(j, half):
+            if half == 0:
+                dn_scaled[j] = scaled.tile([P, D], F32, name="dn_scaled")
+            bank = dn_banks.pop((j, half))[:].rearrange("p (a r m) -> p a m r", a=2, r=2)
+            for a in range(2):
+                cols = slice(W * half + 2 * P * a, W * half + 2 * P * (a + 1))
+                nc.vector.scalar_tensor_tensor(
+                    out=dn_scaled[j][:, cols].rearrange("p (m r) -> p m r", r=2),
+                    in0=bank[:, a],
+                    scalar=rstd_sb[:, j : j + 1],
+                    in1=gain_row[:, cols].rearrange("p (m r) -> p m r", r=2),
+                    op0=MULT,
+                    op1=MULT,
+                )
+
+        def row_sum(j, half):
+            if half == 0:
+                dx_tiles[j] = new_result()
             nc.vector.scalar_tensor_tensor(
-                out=tt[j][:, cols],
-                in0=dn.pop((j, dh))[:],
-                scalar=r_sb[:, j : j + 1],
-                in1=g_row[:, cols],
+                out=dx_tiles[j][:, half_cols(half)],
+                in0=dn_scaled[j][:, half_cols(half)],
+                scalar=mean_factor[:, j : j + 1],
+                in1=x_sb[half][:, j, :],
                 op0=MULT,
                 op1=MULT,
+                accum_out=row_parts[:, j, half : half + 1],
             )
 
-        def E2(j, dh):
-            cols = slice(W * dh, W * (dh + 1))
-            if dh == 0:
-                dx[j] = outs.tile([P, D], F32, name="res", tag="res")
-            nc.vector.scalar_tensor_tensor(
-                out=dx[j][:, cols],
-                in0=tt[j][:, cols],
-                scalar=neg_r2[:, j : j + 1],
-                in1=x_sb[dh][:, j, :],
-                op0=MULT,
-                op1=MULT,
-                accum_out=part[:, j, dh : dh + 1],
+        def join_row_sums(j):
+            nc.vector.tensor_tensor(
+                out=row_terms[:, j : j + 1], in0=row_parts[:, j, 0:1], in1=row_parts[:, j, 1:2], op=ADD
             )
 
-        def EA(j):
-            nc.vector.tensor_tensor(out=cc[:, j : j + 1], in0=part[:, j, 0:1], in1=part[:, j, 1:2], op=ADD)
-
-        def E3(j, dh):
-            cols = slice(W * dh, W * (dh + 1))
+        def dx_half(j, half):
+            cols = half_cols(half)
             nc.vector.scalar_tensor_tensor(
-                out=dx[j][:, cols],
-                in0=x_sb[dh][:, j, :],
-                scalar=cc[:, j : j + 1],
-                in1=tt[j][:, cols],
+                out=dx_tiles[j][:, cols],
+                in0=x_sb[half][:, j, :],
+                scalar=row_terms[:, j : j + 1],
+                in1=dn_scaled[j][:, cols],
                 op0=MULT,
                 op1=ADD,
             )
-            if dh == 1:
-                nc.sync.dma_start(out=out_0.rearrange("b (q j) d -> (b q) j d", j=PACK)[:, j, :], in_=dx.pop(j)[:])
+            nc.sync.dma_start(out=dx_rows[:, j, cols], in_=dx_tiles[j][:, cols])
 
-        load_small()
+        nc.sync.dma_start(out=gain_col[:], in_=g1.rearrange("(p i) -> p i", p=P))
+        nc.sync.dma_start(out=rstd_sb[:], in_=rstd.rearrange("b (q j) -> (b q) j", j=PACK))
         load_x(0)
         load_w(0)
         load_dz(0)
@@ -350,143 +320,96 @@ def tile_transformerblock_pa_v_kernel(
         load_w(1)
         load_dz(3)
         load_w(2)
-        load_dz(4)
-        load_dz(5)
         load_w(3)
+        load_dz(4)
+
         spread_gain()
-        N(0)
-        NI(0)
-        C12(0,ACT)
-        C3(0)
-        QN(0)
-        A(0)
-        TW(0)
-        C12(1,ACT)
-        C3(1)
-        QA(0)
-        row_factor()
-        A(1)
-        TW(1)
+        for j in range(PACK):
+            normed_rows(0, j)
+        interleave_n(0)
+        swap_out(0)
+        swap_in(0)
+        quantise_n(0)
+        interleave_dz(0)
+        transpose_w(0)
+        swap_out(1)
+        swap_in(1)
+        quantise_dz_tok(0)
+        make_mean_factor()
+        interleave_dz(1)
+        transpose_w(1)
         load_w(4)
-        C12(2,ACT)
-        NP(1,0)
-        QA(1)
-        NP(1,1)
-        NP(1,2)
-        NP(1,3)
-        DH(0,0)
-        DH(1,0)
-        C12(3,ACT)
-        DH(2,0)
-        DH(3,0)
-        TW(2)
-        DH(0,1)
-        DH(1,1)
-        TW(3)
+        load_dz(5)
+        swap_out(2)
+        normed_rows(1, 0)
+        quantise_dz_tok(1)
+        for j in range(1, PACK):
+            normed_rows(1, j)
+
+        dw_half(0, 0)
+        dw_half(1, 0)
+        swap_out(3)
+        dw_half(2, 0)
+        dw_half(3, 0)
+        transpose_w(2)
+        dw_half(0, 1)
+        dw_half(1, 1)
+        transpose_w(3)
         load_w(5)
-        DH(2,1)
-        DH(3,1)
-        QW(0)
-        NI(1)
-        QW(1)
-        QN(1)
-        C3(2)
-        C3(3)
-        QW(2)
-        TW(4)
-        DW(4)
-        C12(4,ACT)
-        TW(5)
-        A(2)
-        QW(3)
-        QA(2)
-        DW(5,DVE)
-        C12(5,ACT)
-        QW(4)
-        A(3)
-        C3(4)
-        QA(3)
-        TW(6)
-        DW(6)
-        TW(7)
-        QW(5)
-        C3(5)
-        DW(7,DVE)
-        FJ(0)
-        QW(6)
-        TW(8)
-        DW(8)
-        TW(9)
-        FJ(1)
-        QW(7)
-        DW(9,DVE)
-        QW(8)
-        A(4)
-        TZJ(0)
-        DW(10)
-        TW(10)
-        DW(11)
-        TW(11)
-        QW(9)
-        QTJ(0)
-        QA(4)
-        FJ(2)
-        QW(10)
-        A(5)
-        QW(11)
-        QA(5)
-        MJ(0,0)
-        TZJ(1)
-        DW(12)
-        E1(0,0)
-        FJ(3)
-        E2(0,0)
-        QTJ(1)
-        MJ(0,1)
-        DW(13)
-        DW(14)
-        TZJ(2)
-        DW(15)
-        E1(0,1)
-        E2(0,1)
-        QTJ(2)
-        EA(0)
-        MJ(1,0)
-        DW(16)
-        E1(1,0)
-        E3(0,0)
-        E2(1,0)
-        E3(0,1)
-        MJ(1,1)
-        TZJ(3)
-        DW(17)
-        DW(18)
-        E1(1,1)
-        QTJ(3)
-        E2(1,1)
-        MJ(2,0)
-        DW(19)
-        E1(2,0)
-        EA(1)
-        E2(2,0)
-        E3(1,0)
-        E3(1,1)
-        MJ(2,1)
-        DW(20)
-        DW(21)
-        E1(2,1)
-        MJ(3,0)
-        E2(2,1)
-        E1(3,0)
-        EA(2)
-        E2(3,0)
-        E3(2,0)
-        MJ(3,1)
-        DW(22)
-        E3(2,1)
-        DW(23)
-        E1(3,1)
-        E2(3,1)
-        EA(3)
-        E3(3,0)
-        E3(3,1)
+        dw_half(2, 1)
+        dw_half(3, 1)
+        for k in range(4):
+            store_dw(k)
+        quantise_w(0)
+        interleave_n(1)
+        quantise_w(1)
+        quantise_n(1)
+        swap_in(2)
+        swap_in(3)
+
+        ahead = {
+            4: [(interleave_dz, 2)],
+            5: [(quantise_dz_tok, 2), (interleave_dz, 3)],
+            6: [(quantise_dz_tok, 3)],
+            7: [(sort_dz_pairs, 0)],
+            8: [(sort_dz_pairs, 1)],
+            9: [(interleave_dz, 4)],
+            10: [(quantise_dz_tok, 4), (quantise_dz_feat, 0)],
+            11: [(interleave_dz, 5)],
+        }
+        for u in range(4, W_PIECES):
+            if u == W_PIECES - 2:
+                transpose_dz(0)
+            transpose_w(u)
+            quantise_w(u - 2)
+            for step, index in ahead[u]:
+                step(index)
+            dw_tile(u)
+        quantise_w(W_PIECES - 2)
+        quantise_dz_tok(CHUNKS - 1)
+        quantise_w(W_PIECES - 1)
+
+        for j in range(PACK):
+            k = W_PIECES + 3 * j
+            dn_half(j, 0)
+            if j + 1 < PACK:
+                transpose_dz(j + 1)
+            dw_tile(k)
+            scale_dn(j, 0)
+            if j > 0:
+                dx_half(j - 1, 0)
+            row_sum(j, 0)
+            if j > 0:
+                dx_half(j - 1, 1)
+            if j + 1 < PACK:
+                quantise_dz_feat(j + 1)
+            dn_half(j, 1)
+            dw_tile(k + 1)
+            dw_tile(k + 2)
+            scale_dn(j, 1)
+            if j + 2 < PACK:
+                sort_dz_pairs(j + 2)
+            row_sum(j, 1)
+            join_row_sums(j)
+        dx_half(PACK - 1, 0)
+        dx_half(PACK - 1, 1)

@@ -25,6 +25,7 @@ BATCH_ROWS = P // B
 CHUNKS = 6
 SWAPPED = 4
 W_PIECES = 2 * CHUNKS
+WHOLE_BLOCKS = 8
 VECTOR_DW_TILES = (5, 7, 9)
 
 
@@ -40,12 +41,13 @@ def tile_transformerblock_pa_v_kernel(
 
     with ExitStack() as ctx:
         keep = ctx.enter_context(tc.tile_pool(name="keep", bufs=1))
-        w_loads = ctx.enter_context(tc.tile_pool(name="w_loads", bufs=4))
+        w_loads = ctx.enter_context(tc.tile_pool(name="w_loads", bufs=3))
         stage = ctx.enter_context(tc.tile_pool(name="stage", bufs=8))
         wide = ctx.enter_context(tc.tile_pool(name="wide", bufs=3))
         parking = ctx.enter_context(tc.tile_pool(name="parking", bufs=2))
         scaled = ctx.enter_context(tc.tile_pool(name="scaled", bufs=2))
-        results = ctx.enter_context(tc.tile_pool(name="results", bufs=10))
+        dw_out = ctx.enter_context(tc.tile_pool(name="dw_out", bufs=5))
+        dx_out = ctx.enter_context(tc.tile_pool(name="dx_out", bufs=3))
         psum = ctx.enter_context(tc.psum_pool(name="psum", bufs=8))
         ctx.enter_context(tc.manual_schedule())
 
@@ -60,9 +62,6 @@ def tile_transformerblock_pa_v_kernel(
 
         def new_bank():
             return psum.tile([P, W], F32, name="bank")
-
-        def new_result():
-            return results.tile([P, D], F32, name="result")
 
         ident = keep.tile([P, P], F32)
         make_identity(nc, ident[:])
@@ -146,13 +145,6 @@ def tile_transformerblock_pa_v_kernel(
                 first = first + width
             quantised[key] = (codes, scales)
 
-        def tokens_side_by_side(key, rows, groups):
-            pending[key] = new_stage()
-            nc.vector.tensor_copy(
-                out=pending[key][:].rearrange("p (g m i j) -> p g m j i", g=groups, i=4, j=PACK),
-                in_=rows.rearrange("p (g j m i) -> p g m j i", g=groups, j=PACK, i=4),
-            )
-
         def normed_rows(half, j):
             if j == 0:
                 pending["n_rows", half] = new_stage()
@@ -166,10 +158,19 @@ def tile_transformerblock_pa_v_kernel(
             )
 
         def interleave_n(half):
-            tokens_side_by_side(("n", half), pending.pop(("n_rows", half))[:], 1)
+            rows = pending.pop(("n_rows", half))[:].rearrange("p (j a m i r) -> p a r m j i", j=PACK, a=2, i=4, r=2)
+            pending["n", half] = new_stage()
+            dst = pending["n", half][:].rearrange("p (a r m i j) -> p a r m j i", a=2, r=2, i=4, j=PACK)
+            for a in range(2):
+                nc.vector.tensor_copy(out=dst[:, a], in_=rows[:, a])
 
         def interleave_dz(c):
-            tokens_side_by_side(("dz_tok", c), dz_raw[:, PACK * W * c : PACK * W * (c + 1)], 4)
+            rows = dz_raw[:, PACK * W * c : PACK * W * (c + 1)]
+            pending["dz_tok", c] = new_stage()
+            nc.vector.tensor_copy(
+                out=pending["dz_tok", c][:].rearrange("p (h m i j) -> p h m j i", h=4, i=4, j=PACK),
+                in_=rows.rearrange("p (h j m i) -> p h m j i", h=4, j=PACK, i=4),
+            )
 
         def quantise_n(half):
             quantise(("n", half), E4M3)
@@ -227,30 +228,34 @@ def tile_transformerblock_pa_v_kernel(
                 stop=stop,
             )
 
-        dw_tiles = {}
+        dw_blocks = {}
 
         def dw_half(k, side):
             i, row_tile = divmod(k, 8)
             half, tile = divmod(row_tile, 4)
-            if side == 0:
-                dw_tiles[k] = new_result()
+            if side == 0 and k % 2 == 0:
+                dw_blocks[k // 2] = dw_out.tile([P, 2, D], F32, name="dw_block")
             bank = new_bank()
             mx_pass(bank, quantised["n", half], E4M3, tile, quantised["dz_tok", 2 * i + side], E5M2, True, True)
-            dst = dw_tiles[k][:, half_cols(side)].rearrange("p (a s k) -> p s a k", a=2, s=2)
+            dst = dw_blocks[k // 2][:, k % 2, half_cols(side)].rearrange("p (a s k) -> p s a k", a=2, s=2)
             src = bank[:].rearrange("p (s a k) -> p s a k", s=2, a=2)
             if k in VECTOR_DW_TILES:
                 nc.vector.tensor_copy(out=dst, in_=src)
             else:
                 nc.scalar.copy(out=dst, in_=src)
 
-        def store_dw(k):
-            i, row_tile = divmod(k, 8)
-            nc.sync.dma_start(out=dws[i][P * row_tile : P * (row_tile + 1), :], in_=dw_tiles.pop(k)[:])
+        def store_dw(n, tiles=slice(0, 2)):
+            i, block = divmod(n, 4)
+            rows = dws[i][2 * P * block : 2 * P * (block + 1), :].rearrange("(p r) f -> p r f", r=2)
+            nc.sync.dma_start(out=rows[:, tiles], in_=dw_blocks[n][:, tiles])
 
         def dw_tile(k):
             dw_half(k, 0)
             dw_half(k, 1)
-            store_dw(k)
+            if k // 2 >= WHOLE_BLOCKS:
+                store_dw(k // 2, slice(k % 2, k % 2 + 1))
+            elif k % 2 == 1:
+                store_dw(k // 2)
 
         dn_banks = {}
         dn_scaled = {}
@@ -281,7 +286,7 @@ def tile_transformerblock_pa_v_kernel(
 
         def row_sum(j, half):
             if half == 0:
-                dx_tiles[j] = new_result()
+                dx_tiles[j] = dx_out.tile([P, D], F32, name="dx_tile")
             nc.vector.scalar_tensor_tensor(
                 out=dx_tiles[j][:, half_cols(half)],
                 in0=dn_scaled[j][:, half_cols(half)],
@@ -307,7 +312,10 @@ def tile_transformerblock_pa_v_kernel(
                 op0=MULT,
                 op1=ADD,
             )
-            nc.sync.dma_start(out=dx_rows[:, j, cols], in_=dx_tiles[j][:, cols])
+            if j == PACK - 1:
+                nc.sync.dma_start(out=dx_rows[:, j, cols], in_=dx_tiles[j][:, cols])
+            elif half == 1:
+                nc.sync.dma_start(out=dx_rows[:, j, :], in_=dx_tiles[j][:])
 
         nc.sync.dma_start(out=gain_col[:], in_=g1.rearrange("(p i) -> p i", p=P))
         nc.sync.dma_start(out=rstd_sb[:], in_=rstd.rearrange("b (q j) -> (b q) j", j=PACK))
@@ -320,8 +328,6 @@ def tile_transformerblock_pa_v_kernel(
         load_w(1)
         load_dz(3)
         load_w(2)
-        load_w(3)
-        load_dz(4)
 
         spread_gain()
         for j in range(PACK):
@@ -338,8 +344,8 @@ def tile_transformerblock_pa_v_kernel(
         make_mean_factor()
         interleave_dz(1)
         transpose_w(1)
-        load_w(4)
-        load_dz(5)
+        load_w(3)
+        load_dz(4)
         swap_out(2)
         normed_rows(1, 0)
         quantise_dz_tok(1)
@@ -355,11 +361,10 @@ def tile_transformerblock_pa_v_kernel(
         dw_half(0, 1)
         dw_half(1, 1)
         transpose_w(3)
-        load_w(5)
+        load_w(4)
+        load_dz(5)
         dw_half(2, 1)
         dw_half(3, 1)
-        for k in range(4):
-            store_dw(k)
         quantise_w(0)
         interleave_n(1)
         quantise_w(1)
@@ -381,6 +386,10 @@ def tile_transformerblock_pa_v_kernel(
             if u == W_PIECES - 2:
                 transpose_dz(0)
             transpose_w(u)
+            if u == CHUNKS - 1:
+                load_w(5)
+                store_dw(0)
+                store_dw(1)
             quantise_w(u - 2)
             for step, index in ahead[u]:
                 step(index)

from contextlib import ExitStack

import concourse.mybir as mybir
from concourse.masks import make_identity

B, S, D, H, DK = 2, 256, 1024, 8, 128
T = B * S
FLOPS = 2 * 2 * T * D * 3 * D
BYTES = 2 * T * D + 2 * D + 3 * 2 * D * D + 4 * T + 3 * 2 * T * D + 4 * T * D + 3 * 4 * D * D

F32 = mybir.dt.float32
BF16 = mybir.dt.bfloat16
U32 = mybir.dt.uint32
I32 = mybir.dt.int32
U8 = mybir.dt.uint8
E4M3 = mybir.dt.float8_e4m3fn_x4
E5M2 = mybir.dt.float8_e5m2_x4
MULT = mybir.AluOpType.mult
ADD = mybir.AluOpType.add

P = 128
PACK = 4
W = P * PACK
BATCH_ROWS = P // B
CHUNKS = 6
SWAPPED = 4
W_PIECES = 2 * CHUNKS
WHOLE_BLOCKS = 8
VECTOR_DW_TILES = (5, 7, 9)


def tile_transformerblock_pa_v_kernel(
    tc, x, g1, wq, bq, wk, bk, wv, bv, rstd, grad_0, grad_1, grad_2, out_0, out_1, out_2, out_3
):
    nc = tc.nc
    grads = [grad_0, grad_1, grad_2]
    weights = [wq, wk, wv]
    dws = [out_1, out_2, out_3]
    x_rows = x.rearrange("b (q j) d -> (b q) j d", j=PACK)
    dx_rows = out_0.rearrange("b (q j) d -> (b q) j d", j=PACK)

    with ExitStack() as ctx:
        keep = ctx.enter_context(tc.tile_pool(name="keep", bufs=1))
        w_loads = ctx.enter_context(tc.tile_pool(name="w_loads", bufs=3))
        stage = ctx.enter_context(tc.tile_pool(name="stage", bufs=8))
        wide = ctx.enter_context(tc.tile_pool(name="wide", bufs=3))
        parking = ctx.enter_context(tc.tile_pool(name="parking", bufs=2))
        scaled = ctx.enter_context(tc.tile_pool(name="scaled", bufs=2))
        dw_out = ctx.enter_context(tc.tile_pool(name="dw_out", bufs=5))
        dx_out = ctx.enter_context(tc.tile_pool(name="dx_out", bufs=3))
        psum = ctx.enter_context(tc.psum_pool(name="psum", bufs=8))
        ctx.enter_context(tc.manual_schedule())

        def half_cols(half):
            return slice(W * half, W * (half + 1))

        def new_stage():
            return stage.tile([P, PACK * W], BF16, name="staged", align_bytes=64)

        def new_wide():
            return wide.tile([P, CHUNKS * W], BF16, name="widened", align_bytes=64)

        def new_bank():
            return psum.tile([P, W], F32, name="bank")

        ident = keep.tile([P, P], F32)
        make_identity(nc, ident[:])

        gain_col = keep.tile([P, D // P], BF16)
        rstd_sb = keep.tile([P, PACK], F32)
        x_sb = [keep.tile([P, PACK, W], BF16, name="x_half%d" % half) for half in range(2)]
        dz_raw = keep.tile([P, CHUNKS * PACK * W], BF16)
        w_raw = {}

        def parity_cols(c, s):
            first = PACK * W * c + 2 * W * s
            return dz_raw[:, first : first + 2 * W]

        def load_x(half):
            nc.sync.dma_start(out=x_sb[half][:], in_=x_rows[:, :, half_cols(half)])

        def load_dz(c):
            grad, first_head = grads[c // 2], 4 * (c % 2)
            for b in range(B):
                heads = grad[b, first_head : first_head + 4]
                if c < SWAPPED:
                    src = heads.rearrange("(a s) (q j) k -> (s q) a (j k)", s=2, j=PACK)
                    nc.sync.dma_start(out=parity_cols(c, b).rearrange("p (a r) -> p a r", a=2), in_=src)
                else:
                    src = heads.rearrange("(a s) (q j) k -> s q a (j k)", s=2, j=PACK)
                    rows = slice(BATCH_ROWS * b, BATCH_ROWS * (b + 1))
                    for s in range(2):
                        nc.sync.dma_start(out=parity_cols(c, s).rearrange("p (a r) -> p a r", a=2)[rows], in_=src[s])

        def load_w(n):
            half, i = divmod(n, 3)
            w_raw[n] = w_loads.tile([P, 2, 2 * D], BF16, name="w_rows")
            src = weights[i][half_cols(half), :].rearrange("(a p r) f -> p a (r f)", a=2, r=2)
            nc.sync.dma_start(out=w_raw[n][:], in_=src)

        parked = {}

        def swap_out(c):
            parked[c] = parking.tile([P, W], F32, name="parked")
            even, odd = parity_cols(c, 0).bitcast(F32), parity_cols(c, 1).bitcast(F32)
            nc.scalar.copy(out=parked[c][:BATCH_ROWS], in_=even[BATCH_ROWS:])
            nc.scalar.copy(out=even[BATCH_ROWS:], in_=odd[:BATCH_ROWS])

        def swap_in(c):
            nc.vector.tensor_copy(out=parity_cols(c, 1).bitcast(F32)[:BATCH_ROWS], in_=parked.pop(c)[:BATCH_ROWS])

        gain_row = keep.tile([P, D], BF16)
        mean_factor = keep.tile([P, PACK], F32)

        def spread_gain():
            pairs = gain_col[:].bitcast(F32)
            bank = new_bank()
            for i in range(4):
                nc.tensor.transpose(bank[:, P * i : P * (i + 1)], pairs[:, i : i + 1].to_broadcast([P, P]), ident[:])
            nc.scalar.copy(
                out=gain_row[:].bitcast(F32).rearrange("p (m i) -> p m i", i=4),
                in_=bank[:].rearrange("p (i m) -> p m i", i=4),
            )

        def make_mean_factor():
            nc.vector.scalar_tensor_tensor(
                out=mean_factor[:], in0=rstd_sb[:], scalar=-1.0 / D, in1=rstd_sb[:], op0=MULT, op1=MULT
            )

        pending = {}
        quantised = {}

        def quantise(key, fmt, widths=(W,)):
            src = pending.pop(key)
            codes = keep.tile([P, sum(widths)], U32, name="codes_%s%d" % key, align_bytes=64)
            scales = keep.tile([P, sum(widths)], U8, name="scales_%s%d" % key, align_bytes=64)
            first = 0
            for width in widths:
                cols = slice(first, first + width)
                nc.vector.quantize_mx(
                    out=codes[:, cols].bitcast(fmt),
                    scales=scales[:, cols],
                    in_=src[:, PACK * first : PACK * (first + width)],
                )
                first = first + width
            quantised[key] = (codes, scales)

        def normed_rows(half, j):
            if j == 0:
                pending["n_rows", half] = new_stage()
            nc.vector.scalar_tensor_tensor(
                out=pending["n_rows", half][:, W * j : W * (j + 1)],
                in0=x_sb[half][:, j, :],
                scalar=rstd_sb[:, j : j + 1],
                in1=gain_row[:, half_cols(half)],
                op0=MULT,
                op1=MULT,
            )

        def interleave_n(half):
            rows = pending.pop(("n_rows", half))[:].rearrange("p (j a m i r) -> p a r m j i", j=PACK, a=2, i=4, r=2)
            pending["n", half] = new_stage()
            dst = pending["n", half][:].rearrange("p (a r m i j) -> p a r m j i", a=2, r=2, i=4, j=PACK)
            for a in range(2):
                nc.vector.tensor_copy(out=dst[:, a], in_=rows[:, a])

        def interleave_dz(c):
            rows = dz_raw[:, PACK * W * c : PACK * W * (c + 1)]
            pending["dz_tok", c] = new_stage()
            nc.vector.tensor_copy(
                out=pending["dz_tok", c][:].rearrange("p (h m i j) -> p h m j i", h=4, i=4, j=PACK),
                in_=rows.rearrange("p (h j m i) -> p h m j i", h=4, j=PACK, i=4),
            )

        def quantise_n(half):
            quantise(("n", half), E4M3)

        def quantise_dz_tok(c):
            quantise(("dz_tok", c), E5M2)

        def transpose_run(dst, sources):
            for n in range(len(sources) // 4):
                bank = new_bank()
                for slot in range(4):
                    nc.tensor.transpose(bank[:, P * slot : P * (slot + 1)], sources[4 * n + slot], ident[:])
                nc.scalar.copy(
                    out=dst[:].bitcast(F32)[:, W * n : W * (n + 1)].rearrange("p (i m e) -> p i m e", i=2, e=2),
                    in_=bank[:].rearrange("p (i e m) -> p i m e", i=2, e=2),
                )

        def sort_dz_pairs(j):
            pending["dz_sorted", j] = new_wide()
            dst = pending["dz_sorted", j][:].bitcast(I32)
            dst = dst.rearrange("p (c e a s v) -> p e c a s v", c=CHUNKS, e=2, a=2, s=2)
            src = dz_raw[:].bitcast(I32).rearrange("p (c s a j v e) -> p j e c a s v", c=CHUNKS, s=2, a=2, j=PACK, e=2)
            for e in range(2):
                nc.vector.tensor_copy(out=dst[:, e], in_=src[:, j, e])

        def transpose_dz(j):
            pairs = pending.pop(("dz_sorted", j))[:].bitcast(F32)
            pending["dz_feat", j] = new_wide()
            transpose_run(pending["dz_feat", j], [pairs[:, P * i : P * (i + 1)] for i in range(2 * CHUNKS)])

        def quantise_dz_feat(j):
            quantise(("dz_feat", j), E5M2, (4 * P, 2 * P))

        def transpose_w(u):
            pairs = w_raw[u // 2][:].bitcast(F32)
            firsts = [W * r + 2 * P * (u % 2) for r in range(2)]
            pending["w", u] = new_stage()
            transpose_run(
                pending["w", u],
                [pairs[:, a, first + e : first + 2 * P : 2] for a in range(2) for first in firsts for e in range(2)],
            )

        def quantise_w(u):
            quantise(("w", u), E4M3)

        def mx_pass(bank, lhs, lhs_fmt, tile, rhs, rhs_fmt, start, stop):
            cols = slice(P * tile, P * (tile + 1))
            nc.tensor.matmul_mx(
                out=bank[:],
                lhsT=lhs[0][:, cols].bitcast(lhs_fmt),
                lhsT_scale=lhs[1][:, cols],
                rhs=rhs[0][:].bitcast(rhs_fmt),
                rhs_scale=rhs[1][:],
                start=start,
                stop=stop,
            )

        dw_blocks = {}

        def dw_half(k, side):
            i, row_tile = divmod(k, 8)
            half, tile = divmod(row_tile, 4)
            if side == 0 and k % 2 == 0:
                dw_blocks[k // 2] = dw_out.tile([P, 2, D], F32, name="dw_block")
            bank = new_bank()
            mx_pass(bank, quantised["n", half], E4M3, tile, quantised["dz_tok", 2 * i + side], E5M2, True, True)
            dst = dw_blocks[k // 2][:, k % 2, half_cols(side)].rearrange("p (a s k) -> p s a k", a=2, s=2)
            src = bank[:].rearrange("p (s a k) -> p s a k", s=2, a=2)
            if k in VECTOR_DW_TILES:
                nc.vector.tensor_copy(out=dst, in_=src)
            else:
                nc.scalar.copy(out=dst, in_=src)

        def store_dw(n, tiles=slice(0, 2)):
            i, block = divmod(n, 4)
            rows = dws[i][2 * P * block : 2 * P * (block + 1), :].rearrange("(p r) f -> p r f", r=2)
            nc.sync.dma_start(out=rows[:, tiles], in_=dw_blocks[n][:, tiles])

        def dw_tile(k):
            dw_half(k, 0)
            dw_half(k, 1)
            if k // 2 >= WHOLE_BLOCKS:
                store_dw(k // 2, slice(k % 2, k % 2 + 1))
            elif k % 2 == 1:
                store_dw(k // 2)

        dn_banks = {}
        dn_scaled = {}
        dx_tiles = {}
        row_parts = keep.tile([P, PACK, 2], F32)
        row_terms = keep.tile([P, PACK], F32)

        def dn_half(j, half):
            dn_banks[j, half] = new_bank()
            for c in range(CHUNKS):
                w_piece = quantised["w", CHUNKS * half + c]
                mx_pass(dn_banks[j, half], quantised["dz_feat", j], E5M2, c, w_piece, E4M3, c == 0, c == CHUNKS - 1)

        def scale_dn(j, half):
            if half == 0:
                dn_scaled[j] = scaled.tile([P, D], F32, name="dn_scaled")
            bank = dn_banks.pop((j, half))[:].rearrange("p (a r m) -> p a m r", a=2, r=2)
            for a in range(2):
                cols = slice(W * half + 2 * P * a, W * half + 2 * P * (a + 1))
                nc.vector.scalar_tensor_tensor(
                    out=dn_scaled[j][:, cols].rearrange("p (m r) -> p m r", r=2),
                    in0=bank[:, a],
                    scalar=rstd_sb[:, j : j + 1],
                    in1=gain_row[:, cols].rearrange("p (m r) -> p m r", r=2),
                    op0=MULT,
                    op1=MULT,
                )

        def row_sum(j, half):
            if half == 0:
                dx_tiles[j] = dx_out.tile([P, D], F32, name="dx_tile")
            nc.vector.scalar_tensor_tensor(
                out=dx_tiles[j][:, half_cols(half)],
                in0=dn_scaled[j][:, half_cols(half)],
                scalar=mean_factor[:, j : j + 1],
                in1=x_sb[half][:, j, :],
                op0=MULT,
                op1=MULT,
                accum_out=row_parts[:, j, half : half + 1],
            )

        def join_row_sums(j):
            nc.vector.tensor_tensor(
                out=row_terms[:, j : j + 1], in0=row_parts[:, j, 0:1], in1=row_parts[:, j, 1:2], op=ADD
            )

        def dx_half(j, half):
            cols = half_cols(half)
            nc.vector.scalar_tensor_tensor(
                out=dx_tiles[j][:, cols],
                in0=x_sb[half][:, j, :],
                scalar=row_terms[:, j : j + 1],
                in1=dn_scaled[j][:, cols],
                op0=MULT,
                op1=ADD,
            )
            if j == PACK - 1:
                nc.sync.dma_start(out=dx_rows[:, j, cols], in_=dx_tiles[j][:, cols])
            elif half == 1:
                nc.sync.dma_start(out=dx_rows[:, j, :], in_=dx_tiles[j][:])

        nc.sync.dma_start(out=gain_col[:], in_=g1.rearrange("(p i) -> p i", p=P))
        nc.sync.dma_start(out=rstd_sb[:], in_=rstd.rearrange("b (q j) -> (b q) j", j=PACK))
        load_x(0)
        load_w(0)
        load_dz(0)
        load_dz(1)
        load_x(1)
        load_dz(2)
        load_w(1)
        load_dz(3)
        load_w(2)

        spread_gain()
        for j in range(PACK):
            normed_rows(0, j)
        interleave_n(0)
        swap_out(0)
        swap_in(0)
        quantise_n(0)
        interleave_dz(0)
        transpose_w(0)
        swap_out(1)
        swap_in(1)
        quantise_dz_tok(0)
        make_mean_factor()
        interleave_dz(1)
        transpose_w(1)
        load_w(3)
        load_dz(4)
        swap_out(2)
        normed_rows(1, 0)
        quantise_dz_tok(1)
        for j in range(1, PACK):
            normed_rows(1, j)

        dw_half(0, 0)
        dw_half(1, 0)
        swap_out(3)
        dw_half(2, 0)
        dw_half(3, 0)
        transpose_w(2)
        dw_half(0, 1)
        dw_half(1, 1)
        transpose_w(3)
        load_w(4)
        load_dz(5)
        dw_half(2, 1)
        dw_half(3, 1)
        quantise_w(0)
        interleave_n(1)
        quantise_w(1)
        quantise_n(1)
        swap_in(2)
        swap_in(3)

        ahead = {
            4: [(interleave_dz, 2)],
            5: [(quantise_dz_tok, 2), (interleave_dz, 3)],
            6: [(quantise_dz_tok, 3)],
            7: [(sort_dz_pairs, 0)],
            8: [(sort_dz_pairs, 1)],
            9: [(interleave_dz, 4)],
            10: [(quantise_dz_tok, 4), (quantise_dz_feat, 0)],
            11: [(interleave_dz, 5)],
        }
        for u in range(4, W_PIECES):
            if u == W_PIECES - 2:
                transpose_dz(0)
            transpose_w(u)
            if u == CHUNKS - 1:
                load_w(5)
                store_dw(0)
                store_dw(1)
            quantise_w(u - 2)
            for step, index in ahead[u]:
                step(index)
            dw_tile(u)
        quantise_w(W_PIECES - 2)
        quantise_dz_tok(CHUNKS - 1)
        quantise_w(W_PIECES - 1)

        for j in range(PACK):
            k = W_PIECES + 3 * j
            dn_half(j, 0)
            if j + 1 < PACK:
                transpose_dz(j + 1)
            dw_tile(k)
            scale_dn(j, 0)
            if j > 0:
                dx_half(j - 1, 0)
            row_sum(j, 0)
            if j > 0:
                dx_half(j - 1, 1)
            if j + 1 < PACK:
                quantise_dz_feat(j + 1)
            dn_half(j, 1)
            dw_tile(k + 1)
            dw_tile(k + 2)
            scale_dn(j, 1)
            if j + 2 < PACK:
                sort_dz_pairs(j + 2)
            row_sum(j, 1)
            join_row_sums(j)
        dx_half(PACK - 1, 0)
        dx_half(PACK - 1, 1)
